import numpy as np
import ml_dtypes


def mxq(x, axis, fmt="e4m3"):
    dtype, down = {"e4m3": (ml_dtypes.float8_e4m3fn, 7), "e5m2": (ml_dtypes.float8_e5m2, 14)}[fmt]
    v = np.moveaxis(np.asarray(x, np.float32).astype(ml_dtypes.bfloat16).astype(np.float64), axis, -1)
    blocks = v.reshape(v.shape[:-1] + (-1, 32))
    amax = np.abs(blocks).max(-1, keepdims=True)
    byte = np.maximum(np.where(amax > 0, np.frexp(amax)[1] - 1 + 127, 0) - down, 1)
    scale = np.exp2(byte - 127.0)
    codes = (blocks / scale).astype(np.float32).astype(dtype).astype(np.float64)
    return np.moveaxis((codes * scale).reshape(v.shape), -1, axis)


WIDE = False


def mx_kscale(k):
    if not WIDE:
        return np.ones(k)
    levels = np.array([10, -10, 5, -5, 0])
    a = np.random.permutation(np.resize(levels, k // 512 * 4)).reshape(k // 512, 4)
    idx = np.arange(k)
    return np.exp2(a[idx // 512, idx % 128 // 32])


BF16 = ml_dtypes.bfloat16


def bf(x):
    return np.asarray(x, np.float32).astype(BF16)


def f64(x):
    return np.asarray(x).astype(np.float64)


N, D, DO, R0, R1, R2, R3, R4 = 1536, 8192, 128, 1, 2, 4, 12, 25
SCALES = (R0, R1, R2, R3)
NS = len(SCALES)


def setup_inputs():
    s = mx_kscale(D)
    return {"inputs_c_e": bf(np.random.standard_normal((N, D)) * s),
            "Ws": bf(np.random.standard_normal((NS, DO, D)) / np.sqrt(D) / s),
            "bs": bf(np.random.standard_normal((NS, DO)) * 0.5)}


def reference(inputs_c_e, Ws, bs):
    x, W, b = f64(inputs_c_e), f64(Ws), f64(bs)
    outs = []
    for i, r in enumerate(SCALES):
        groups = N // r
        sums = x.reshape(groups, r, D).sum(axis=1)
        h = np.maximum((mxq(sums, 1, "e4m3") @ mxq(W[i].T, 0, "e4m3")) + b[i], 0.0) / r
        outs.append(np.repeat(h, r, axis=0))
    return np.concatenate(outs, axis=0)

@@ -1,0 +1,222 @@
+import concourse.mybir as mybir
+from concourse.masks import make_identity
+
+F32 = mybir.dt.float32
+BF16 = mybir.dt.bfloat16
+U32 = mybir.dt.uint32
+U8 = mybir.dt.uint8
+FP8X4 = mybir.dt.float8_e4m3fn_x4
+ADD = mybir.AluOpType.add
+RELU = mybir.ActivationFunctionType.Relu
+
+P = 128
+N_ROWS = 1536
+D = 8192
+SCALES = (1, 2, 4, 12)
+GROUP = 12
+QUAD = 4
+N_BLOCKS = GROUP // QUAD
+PACK = 4
+K_PASS = P * PACK
+N_PASSES = D // K_PASS
+UNIT_PASSES = 2
+K_UNIT = UNIT_PASSES * K_PASS
+N_UNITS = D // K_UNIT
+PLANE = P * PACK
+
+FLOPS = 2 * sum(N_ROWS // r for r in SCALES) * D * P
+
+
+def tile_contractexpand_pa_k_kernel(tc, inputs_c_e, Ws, bs, out):
+    nc = tc.nc
+    x_rows = inputs_c_e.rearrange("(c j) k -> c j k", j=GROUP)
+    w_rows = Ws.rearrange("i o k -> o i k")
+    out_rows = out.rearrange("(i c j) o -> c i j o", i=len(SCALES), j=GROUP)
+
+    units = []
+    for h in range(N_UNITS):
+        units.append(("w", 0, h))
+        units.append(("x", 0, h))
+    for b in range(1, N_BLOCKS):
+        for h in range(N_UNITS):
+            units.append(("x", b, h))
+
+    with tc.tile_pool(name="keep", bufs=1) as keep, tc.tile_pool(name="raw", bufs=3) as raw_pool, tc.tile_pool(
+        name="work", bufs=2
+    ) as work, tc.psum_pool(name="flip", bufs=4) as flip_pool, tc.psum_pool(name="acc", bufs=1) as acc_pool:
+        identity = keep.tile([P, P], F32, name="identity")
+        make_identity(nc, identity[:])
+
+        w_codes = keep.tile([P, N_PASSES, len(SCALES), P], U32, name="w_codes", align_bytes=64)
+        w_scales = keep.tile([P, N_PASSES, len(SCALES), P], U8, name="w_scales", align_bytes=64)
+        run12 = keep.tile([P, N_PASSES, PLANE], F32, name="run12")
+
+        bias_rows = keep.tile([P, P], BF16, name="bias_rows")
+        nc.vector.memset(bias_rows[:], 0.0)
+        nc.sync.dma_start(out=bias_rows[0 : len(SCALES), :], in_=bs)
+        bias_wide = keep.tile([P, P], F32, name="bias_wide")
+        nc.vector.tensor_copy(out=bias_wide[:], in_=bias_rows[:])
+        bias_bank = flip_pool.tile([P, 2, 2, P], F32, name="bank")
+        nc.tensor.transpose(bias_bank[:, 0, 0, :], bias_wide[:], identity[:])
+        bias = keep.tile([P, len(SCALES)], F32, name="bias")
+        nc.vector.tensor_copy(out=bias[:], in_=bias_bank[:, 0, 0, 0 : len(SCALES)])
+
+        raws = {}
+        banks = {}
+        groupeds = {}
+        accs = {}
+
+        def load(n):
+            kind, b, h = units[n]
+            k_cols = slice(h * K_UNIT, (h + 1) * K_UNIT)
+            raw = raw_pool.tile([P, QUAD, K_UNIT], BF16, name="raw")
+            if kind == "w":
+                nc.sync.dma_start(out=raw[:], in_=w_rows[:, :, k_cols])
+            else:
+                nc.sync.dma_start(out=raw[:], in_=x_rows[:, b * QUAD : (b + 1) * QUAD, k_cols])
+            raws[n] = raw
+
+        def transpose(n):
+            words = raws[n][:].bitcast(F32)
+            banks[n] = []
+            for q in range(UNIT_PASSES):
+                for pair in range(QUAD // 2):
+                    bank = flip_pool.tile([P, 2, 2, P], F32, name="bank")
+                    for s in range(2):
+                        for u in range(2):
+                            first = (2 * q + u) * P
+                            nc.tensor.transpose(
+                                bank[:, s, u, :], words[:, 2 * pair + s, first : first + P], identity[:]
+                            )
+                    banks[n].append(bank)
+
+        def copy_out(n):
+            grouped = work.tile([P, UNIT_PASSES, QUAD, PLANE], BF16, name="grouped", align_bytes=64, bufs=3)
+            words = grouped[:].bitcast(F32).rearrange("w q s (c u) -> w q s c u", u=2)
+            for q in range(UNIT_PASSES):
+                for pair in range(QUAD // 2):
+                    bank = banks[n][q * (QUAD // 2) + pair]
+                    nc.scalar.copy(
+                        out=words[:, q, 2 * pair : 2 * pair + 2, :, :],
+                        in_=bank[:].rearrange("w s u c -> w s c u"),
+                    )
+            groupeds[n] = grouped
+
+        def quantise(values, name):
+            width = values.shape[1] // PACK
+            codes = work.tile([P, width], U32, name=name + "_codes", align_bytes=64)
+            scales = work.tile([P, width], U8, name=name + "_scales", align_bytes=64)
+            nc.vector.quantize_mx(out=codes[:].bitcast(FP8X4), scales=scales[:], in_=values)
+            return codes, scales
+
+        def multiply(i, g, operand, q):
+            codes, scales = operand
+            width = codes.shape[1] // UNIT_PASSES
+            cols = slice(q * width, (q + 1) * width)
+            nc.tensor.matmul_mx(
+                out=accs[i][:],
+                lhsT=w_codes[:, g, i, :].bitcast(FP8X4),
+                lhsT_scale=w_scales[:, g, i, :],
+                rhs=codes[:, cols].bitcast(FP8X4),
+                rhs_scale=scales[:, cols],
+                start=(g == 0),
+                stop=(g == N_PASSES - 1),
+            )
+
+        def quantise_weights(n):
+            h = units[n][2]
+            passes = slice(h * UNIT_PASSES, (h + 1) * UNIT_PASSES)
+            nc.vector.quantize_mx(
+                out=w_codes[:, passes, :, :].rearrange("w g i o -> w (g i o)").bitcast(FP8X4),
+                scales=w_scales[:, passes, :, :].rearrange("w g i o -> w (g i o)"),
+                in_=groupeds[n][:].rearrange("w q s v -> w (q s v)"),
+            )
+
+        def sum_quantise_multiply(n):
+            b, h = units[n][1], units[n][2]
+            passes = slice(h * UNIT_PASSES, (h + 1) * UNIT_PASSES)
+            grouped = groupeds[n]
+
+            pairs = grouped[:].rearrange("w q (m two) v -> w (q m) two v", two=2)
+            sum2 = work.tile([P, UNIT_PASSES * 2, PLANE], F32, name="sum2")
+            nc.vector.tensor_tensor(out=sum2[:], in0=pairs[:, :, 0, :], in1=pairs[:, :, 1, :], op=ADD)
+            halves = sum2[:].rearrange("w (q m) v -> w q m v", m=2)
+            if b == 0:
+                sum4 = run12[:, passes, :]
+            else:
+                sum4_tile = work.tile([P, UNIT_PASSES, PLANE], F32, name="sum4")
+                sum4 = sum4_tile[:]
+            nc.vector.tensor_tensor(out=sum4, in0=halves[:, :, 0, :], in1=halves[:, :, 1, :], op=ADD)
+
+            sum2_bf = work.tile([P, UNIT_PASSES * 2, PLANE], BF16, name="sum2_bf", align_bytes=64)
+            nc.scalar.copy(out=sum2_bf[:], in_=sum2[:])
+            sum4_bf = work.tile([P, UNIT_PASSES, PLANE], BF16, name="sum4_bf", align_bytes=64)
+            nc.scalar.copy(out=sum4_bf[:], in_=sum4)
+
+            if b == 1:
+                nc.vector.tensor_tensor(out=run12[:, passes, :], in0=run12[:, passes, :], in1=sum4, op=ADD)
+            if b == N_BLOCKS - 1:
+                sum12_bf = work.tile([P, UNIT_PASSES, PLANE], BF16, name="sum12_bf", align_bytes=64)
+                nc.vector.tensor_tensor(out=sum12_bf[:], in0=run12[:, passes, :], in1=sum4, op=ADD)
+
+            operands = [
+                quantise(grouped[:].rearrange("w q s v -> w (q s v)"), "x"),
+                quantise(sum2_bf[:].rearrange("w a v -> w (a v)"), "sum2"),
+                quantise(sum4_bf[:].rearrange("w q v -> w (q v)"), "sum4"),
+            ]
+            if b == N_BLOCKS - 1:
+                operands.append(quantise(sum12_bf[:].rearrange("w q v -> w (q v)"), "sum12"))
+
+            for q in range(UNIT_PASSES):
+                for i in range(len(operands)):
+                    multiply(i, h * UNIT_PASSES + q, operands[i], q)
+
+        def open_accumulator(i):
+            planes = max(QUAD // SCALES[i], 1)
+            accs[i] = acc_pool.tile([P, planes * P], F32, name="acc%d" % i, tag="bank%d" % i)
+
+        def finish(i, first_row, n_rows):
+            r = SCALES[i]
+            planes = n_rows // r
+            relu = work.tile([P, planes, P], F32, name="relu%d" % i)
+            nc.scalar.activation(
+                out=relu[:].rearrange("o m c -> o (m c)"), in_=accs[i][:], func=RELU, bias=bias[:, i : i + 1], scale=1.0
+            )
+            back = acc_pool.tile([P, planes, P], F32, name="back%d" % i, tag="bank%d" % i)
+            for m in range(planes):
+                nc.tensor.transpose(back[:, m, :], relu[:, m, :], identity[:])
+            result = work.tile([P, planes, P], F32, name="result%d" % i)
+            nc.scalar.mul(out=result[:], in_=back[:], mul=1.0 / r)
+            for m in range(planes):
+                rows = slice(first_row + m * r, first_row + (m + 1) * r)
+                nc.sync.dma_start(
+                    out=out_rows[:, i, rows, :], in_=result[:, m : m + 1, :].to_broadcast([P, r, P])
+                )
+
+        for n in range(3):
+            load(n)
+        transpose(0)
+        copy_out(0)
+        transpose(1)
+        for n in range(len(units)):
+            kind, b, h = units[n]
+            if n + 3 < len(units):
+                load(n + 3)
+            if n + 1 < len(units):
+                copy_out(n + 1)
+            if kind == "x" and h == 0:
+                for i in range(3):
+                    if b > 0:
+                        finish(i, (b - 1) * QUAD, QUAD)
+                    open_accumulator(i)
+                if b == N_BLOCKS - 1:
+                    open_accumulator(3)
+            if n + 2 < len(units):
+                transpose(n + 2)
+            if kind == "w":
+                quantise_weights(n)
+            else:
+                sum_quantise_multiply(n)
+        for i in range(3):
+            finish(i, (N_BLOCKS - 1) * QUAD, QUAD)
+        finish(3, 0, GROUP)

@@ -20,9 +20,9 @@ PACK = 4
 K_PASS = P * PACK
 N_PASSES = D // K_PASS
 UNIT_PASSES = 2
-K_UNIT = UNIT_PASSES * K_PASS
-N_UNITS = D // K_UNIT
+N_UNITS = N_PASSES // UNIT_PASSES
 PLANE = P * PACK
+UNIT_BANKS = UNIT_PASSES * QUAD // 2
 
 FLOPS = 2 * sum(N_ROWS // r for r in SCALES) * D * P
 
@@ -35,15 +35,15 @@ def tile_contractexpand_pa_k_kernel(tc, inputs_c_e, Ws, bs, out):
 
     units = []
     for h in range(N_UNITS):
-        units.append(("w", 0, h))
         units.append(("x", 0, h))
+        units.append(("w", 0, h))
     for b in range(1, N_BLOCKS):
         for h in range(N_UNITS):
             units.append(("x", b, h))
 
     with tc.tile_pool(name="keep", bufs=1) as keep, tc.tile_pool(name="raw", bufs=3) as raw_pool, tc.tile_pool(
         name="work", bufs=2
-    ) as work, tc.psum_pool(name="flip", bufs=4) as flip_pool, tc.psum_pool(name="acc", bufs=1) as acc_pool:
+    ) as work, tc.psum_pool(name="flip", bufs=UNIT_BANKS) as flip_pool, tc.psum_pool(name="acc", bufs=1) as acc_pool:
         identity = keep.tile([P, P], F32, name="identity")
         make_identity(nc, identity[:])
 
@@ -53,27 +53,30 @@ def tile_contractexpand_pa_k_kernel(tc, inputs_c_e, Ws, bs, out):
 
         bias_rows = keep.tile([P, P], BF16, name="bias_rows")
         nc.vector.memset(bias_rows[:], 0.0)
-        nc.sync.dma_start(out=bias_rows[0 : len(SCALES), :], in_=bs)
+        nc.scalar.dma_start(out=bias_rows[0 : len(SCALES), :], in_=bs)
         bias_wide = keep.tile([P, P], F32, name="bias_wide")
         nc.vector.tensor_copy(out=bias_wide[:], in_=bias_rows[:])
-        bias_bank = flip_pool.tile([P, 2, 2, P], F32, name="bank")
-        nc.tensor.transpose(bias_bank[:, 0, 0, :], bias_wide[:], identity[:])
+        bias_bank = acc_pool.tile([P, P], F32, name="bias_bank", tag="bank3")
+        nc.tensor.transpose(bias_bank[:], bias_wide[:], identity[:])
         bias = keep.tile([P, len(SCALES)], F32, name="bias")
-        nc.vector.tensor_copy(out=bias[:], in_=bias_bank[:, 0, 0, 0 : len(SCALES)])
+        nc.vector.tensor_copy(out=bias[:], in_=bias_bank[:, 0 : len(SCALES)])
 
         raws = {}
         banks = {}
         groupeds = {}
+        operands = {}
         accs = {}
 
         def load(n):
             kind, b, h = units[n]
-            k_cols = slice(h * K_UNIT, (h + 1) * K_UNIT)
-            raw = raw_pool.tile([P, QUAD, K_UNIT], BF16, name="raw")
-            if kind == "w":
-                nc.sync.dma_start(out=raw[:], in_=w_rows[:, :, k_cols])
-            else:
-                nc.sync.dma_start(out=raw[:], in_=x_rows[:, b * QUAD : (b + 1) * QUAD, k_cols])
+            raw = raw_pool.tile([P, UNIT_PASSES, QUAD, K_PASS], BF16, name="raw")
+            for q in range(UNIT_PASSES):
+                g = h * UNIT_PASSES + q
+                k_cols = slice(g * K_PASS, (g + 1) * K_PASS)
+                if kind == "w":
+                    nc.sync.dma_start(out=raw[:, q, :, :], in_=w_rows[:, :, k_cols])
+                else:
+                    nc.sync.dma_start(out=raw[:, q, :, :], in_=x_rows[:, b * QUAD : (b + 1) * QUAD, k_cols])
             raws[n] = raw
 
         def transpose(n):
@@ -84,21 +87,24 @@ def tile_contractexpand_pa_k_kernel(tc, inputs_c_e, Ws, bs, out):
                     bank = flip_pool.tile([P, 2, 2, P], F32, name="bank")
                     for s in range(2):
                         for u in range(2):
-                            first = (2 * q + u) * P
                             nc.tensor.transpose(
-                                bank[:, s, u, :], words[:, 2 * pair + s, first : first + P], identity[:]
+                                bank[:, s, u, :], words[:, q, 2 * pair + s, u * P : (u + 1) * P], identity[:]
                             )
                     banks[n].append(bank)
 
         def copy_out(n):
+            kind, b, h = units[n]
             grouped = work.tile([P, UNIT_PASSES, QUAD, PLANE], BF16, name="grouped", align_bytes=64, bufs=3)
             words = grouped[:].bitcast(F32).rearrange("w q s (c u) -> w q s c u", u=2)
             for q in range(UNIT_PASSES):
                 for pair in range(QUAD // 2):
-                    bank = banks[n][q * (QUAD // 2) + pair]
-                    nc.scalar.copy(
+                    a = q * (QUAD // 2) + pair
+                    copy = nc.scalar.copy
+                    if kind == "x" and b == 0 and a == UNIT_BANKS - 1:
+                        copy = nc.vector.tensor_copy
+                    copy(
                         out=words[:, q, 2 * pair : 2 * pair + 2, :, :],
-                        in_=bank[:].rearrange("w s u c -> w s c u"),
+                        in_=banks[n][a][:].rearrange("w s u c -> w s c u"),
                     )
             groupeds[n] = grouped
 
@@ -109,20 +115,6 @@ def tile_contractexpand_pa_k_kernel(tc, inputs_c_e, Ws, bs, out):
             nc.vector.quantize_mx(out=codes[:].bitcast(FP8X4), scales=scales[:], in_=values)
             return codes, scales
 
-        def multiply(i, g, operand, q):
-            codes, scales = operand
-            width = codes.shape[1] // UNIT_PASSES
-            cols = slice(q * width, (q + 1) * width)
-            nc.tensor.matmul_mx(
-                out=accs[i][:],
-                lhsT=w_codes[:, g, i, :].bitcast(FP8X4),
-                lhsT_scale=w_scales[:, g, i, :],
-                rhs=codes[:, cols].bitcast(FP8X4),
-                rhs_scale=scales[:, cols],
-                start=(g == 0),
-                stop=(g == N_PASSES - 1),
-            )
-
         def quantise_weights(n):
             h = units[n][2]
             passes = slice(h * UNIT_PASSES, (h + 1) * UNIT_PASSES)
@@ -132,7 +124,7 @@ def tile_contractexpand_pa_k_kernel(tc, inputs_c_e, Ws, bs, out):
                 in_=groupeds[n][:].rearrange("w q s v -> w (q s v)"),
             )
 
-        def sum_quantise_multiply(n):
+        def sum_and_quantise(n):
             b, h = units[n][1], units[n][2]
             passes = slice(h * UNIT_PASSES, (h + 1) * UNIT_PASSES)
             grouped = groupeds[n]
@@ -159,64 +151,86 @@ def tile_contractexpand_pa_k_kernel(tc, inputs_c_e, Ws, bs, out):
                 sum12_bf = work.tile([P, UNIT_PASSES, PLANE], BF16, name="sum12_bf", align_bytes=64)
                 nc.vector.tensor_tensor(out=sum12_bf[:], in0=run12[:, passes, :], in1=sum4, op=ADD)
 
-            operands = [
+            operands[n] = [
                 quantise(grouped[:].rearrange("w q s v -> w (q s v)"), "x"),
                 quantise(sum2_bf[:].rearrange("w a v -> w (a v)"), "sum2"),
                 quantise(sum4_bf[:].rearrange("w q v -> w (q v)"), "sum4"),
             ]
             if b == N_BLOCKS - 1:
-                operands.append(quantise(sum12_bf[:].rearrange("w q v -> w (q v)"), "sum12"))
+                operands[n].append(quantise(sum12_bf[:].rearrange("w q v -> w (q v)"), "sum12"))
 
-            for q in range(UNIT_PASSES):
-                for i in range(len(operands)):
-                    multiply(i, h * UNIT_PASSES + q, operands[i], q)
+        def multiply(n):
+            b, h = units[n][1], units[n][2]
+            for i in range(len(operands[n])):
+                if h == 0:
+                    planes = max(QUAD // SCALES[i], 1)
+                    accs[i] = acc_pool.tile([P, planes * P], F32, name="acc%d" % i, tag="bank%d" % i)
+                codes, scales = operands[n][i]
+                width = codes.shape[1] // UNIT_PASSES
+                for q in range(UNIT_PASSES):
+                    g = h * UNIT_PASSES + q
+                    cols = slice(q * width, (q + 1) * width)
+                    nc.tensor.matmul_mx(
+                        out=accs[i][:],
+                        lhsT=w_codes[:, g, i, :].bitcast(FP8X4),
+                        lhsT_scale=w_scales[:, g, i, :],
+                        rhs=codes[:, cols].bitcast(FP8X4),
+                        rhs_scale=scales[:, cols],
+                        start=(g == 0),
+                        stop=(g == N_PASSES - 1),
+                    )
+            if h == N_UNITS - 1:
+                finish(b, len(operands[n]))
 
-        def open_accumulator(i):
-            planes = max(QUAD // SCALES[i], 1)
-            accs[i] = acc_pool.tile([P, planes * P], F32, name="acc%d" % i, tag="bank%d" % i)
-
-        def finish(i, first_row, n_rows):
-            r = SCALES[i]
-            planes = n_rows // r
-            relu = work.tile([P, planes, P], F32, name="relu%d" % i)
-            nc.scalar.activation(
-                out=relu[:].rearrange("o m c -> o (m c)"), in_=accs[i][:], func=RELU, bias=bias[:, i : i + 1], scale=1.0
-            )
-            back = acc_pool.tile([P, planes, P], F32, name="back%d" % i, tag="bank%d" % i)
-            for m in range(planes):
-                nc.tensor.transpose(back[:, m, :], relu[:, m, :], identity[:])
-            result = work.tile([P, planes, P], F32, name="result%d" % i)
-            nc.scalar.mul(out=result[:], in_=back[:], mul=1.0 / r)
-            for m in range(planes):
-                rows = slice(first_row + m * r, first_row + (m + 1) * r)
-                nc.sync.dma_start(
-                    out=out_rows[:, i, rows, :], in_=result[:, m : m + 1, :].to_broadcast([P, r, P])
+        def finish(b, n_scales):
+            relus = []
+            backs = []
+            for i in range(n_scales):
+                planes = accs[i].shape[1] // P
+                relu = work.tile([P, planes, P], F32, name="relu%d" % i)
+                nc.scalar.activation(
+                    out=relu[:].rearrange("o m c -> o (m c)"),
+                    in_=accs[i][:],
+                    func=RELU,
+                    bias=bias[:, i : i + 1],
+                    scale=1.0,
                 )
+                relus.append(relu)
+            for i in range(n_scales):
+                planes = accs[i].shape[1] // P
+                back = acc_pool.tile([P, planes, P], F32, name="back%d" % i, tag="bank%d" % i)
+                for m in range(planes):
+                    nc.tensor.transpose(back[:, m, :], relus[i][:, m, :], identity[:])
+                backs.append(back)
+            for i in range(n_scales):
+                r = SCALES[i]
+                planes = accs[i].shape[1] // P
+                first_row = b * QUAD if r <= QUAD else 0
+                result = work.tile([P, planes, P], F32, name="result%d" % i)
+                nc.scalar.mul(out=result[:], in_=backs[i][:], mul=1.0 / r)
+                for m in range(planes):
+                    rows = slice(first_row + m * r, first_row + (m + 1) * r)
+                    nc.sync.dma_start(
+                        out=out_rows[:, i, rows, :], in_=result[:, m : m + 1, :].to_broadcast([P, r, P])
+                    )
 
-        for n in range(3):
-            load(n)
-        transpose(0)
-        copy_out(0)
-        transpose(1)
-        for n in range(len(units)):
-            kind, b, h = units[n]
-            if n + 3 < len(units):
-                load(n + 3)
-            if n + 1 < len(units):
-                copy_out(n + 1)
-            if kind == "x" and h == 0:
-                for i in range(3):
-                    if b > 0:
-                        finish(i, (b - 1) * QUAD, QUAD)
-                    open_accumulator(i)
-                if b == N_BLOCKS - 1:
-                    open_accumulator(3)
-            if n + 2 < len(units):
-                transpose(n + 2)
-            if kind == "w":
-                quantise_weights(n)
-            else:
-                sum_quantise_multiply(n)
-        for i in range(3):
-            finish(i, (N_BLOCKS - 1) * QUAD, QUAD)
-        finish(3, 0, GROUP)
+        with tc.manual_schedule():
+            for n in range(3):
+                load(n)
+            transpose(0)
+            copy_out(0)
+            transpose(1)
+            for n in range(len(units) + 1):
+                if n + 3 < len(units):
+                    load(n + 3)
+                if n + 1 < len(units):
+                    copy_out(n + 1)
+                if n + 2 < len(units):
+                    transpose(n + 2)
+                if n < len(units):
+                    if units[n][0] == "w":
+                        quantise_weights(n)
+                    else:
+                        sum_and_quantise(n)
+                if n >= 1 and units[n - 1][0] == "x":
+                    multiply(n - 1)

@@ -22,7 +22,7 @@ N_PASSES = D // K_PASS
 UNIT_PASSES = 2
 N_UNITS = N_PASSES // UNIT_PASSES
 PLANE = P * PACK
-UNIT_BANKS = UNIT_PASSES * QUAD // 2
+FLIP_BANKS = 5
 
 FLOPS = 2 * sum(N_ROWS // r for r in SCALES) * D * P
 
@@ -43,7 +43,7 @@ def tile_contractexpand_pa_k_kernel(tc, inputs_c_e, Ws, bs, out):
 
     with tc.tile_pool(name="keep", bufs=1) as keep, tc.tile_pool(name="raw", bufs=3) as raw_pool, tc.tile_pool(
         name="work", bufs=2
-    ) as work, tc.psum_pool(name="flip", bufs=UNIT_BANKS) as flip_pool, tc.psum_pool(name="acc", bufs=1) as acc_pool:
+    ) as work, tc.psum_pool(name="flip", bufs=FLIP_BANKS) as flip_pool, tc.psum_pool(name="acc", bufs=1) as acc_pool:
         identity = keep.tile([P, P], F32, name="identity")
         make_identity(nc, identity[:])
 
@@ -53,10 +53,10 @@ def tile_contractexpand_pa_k_kernel(tc, inputs_c_e, Ws, bs, out):
 
         bias_rows = keep.tile([P, P], BF16, name="bias_rows")
         nc.vector.memset(bias_rows[:], 0.0)
-        nc.scalar.dma_start(out=bias_rows[0 : len(SCALES), :], in_=bs)
+        nc.sync.dma_start(out=bias_rows[0 : len(SCALES), :], in_=bs)
         bias_wide = keep.tile([P, P], F32, name="bias_wide")
         nc.vector.tensor_copy(out=bias_wide[:], in_=bias_rows[:])
-        bias_bank = acc_pool.tile([P, P], F32, name="bias_bank", tag="bank3")
+        bias_bank = flip_pool.tile([P, P], F32, name="bias_bank", tag="bank")
         nc.tensor.transpose(bias_bank[:], bias_wide[:], identity[:])
         bias = keep.tile([P, len(SCALES)], F32, name="bias")
         nc.vector.tensor_copy(out=bias[:], in_=bias_bank[:, 0 : len(SCALES)])
@@ -64,19 +64,23 @@ def tile_contractexpand_pa_k_kernel(tc, inputs_c_e, Ws, bs, out):
         raws = {}
         banks = {}
         groupeds = {}
+        sums2 = {}
+        sums12 = {}
         operands = {}
         accs = {}
 
         def load(n):
             kind, b, h = units[n]
+            source = w_rows if kind == "w" else x_rows
             raw = raw_pool.tile([P, UNIT_PASSES, QUAD, K_PASS], BF16, name="raw")
             for q in range(UNIT_PASSES):
                 g = h * UNIT_PASSES + q
-                k_cols = slice(g * K_PASS, (g + 1) * K_PASS)
-                if kind == "w":
-                    nc.sync.dma_start(out=raw[:, q, :, :], in_=w_rows[:, :, k_cols])
-                else:
-                    nc.sync.dma_start(out=raw[:, q, :, :], in_=x_rows[:, b * QUAD : (b + 1) * QUAD, k_cols])
+                for pair in range(QUAD // 2):
+                    first = b * QUAD + 2 * pair
+                    nc.sync.dma_start(
+                        out=raw[:, q, 2 * pair : 2 * pair + 2, :],
+                        in_=source[:, first : first + 2, g * K_PASS : (g + 1) * K_PASS],
+                    )
             raws[n] = raw
 
         def transpose(n):
@@ -93,20 +97,29 @@ def tile_contractexpand_pa_k_kernel(tc, inputs_c_e, Ws, bs, out):
                     banks[n].append(bank)
 
         def copy_out(n):
-            kind, b, h = units[n]
             grouped = work.tile([P, UNIT_PASSES, QUAD, PLANE], BF16, name="grouped", align_bytes=64, bufs=3)
             words = grouped[:].bitcast(F32).rearrange("w q s (c u) -> w q s c u", u=2)
             for q in range(UNIT_PASSES):
                 for pair in range(QUAD // 2):
-                    a = q * (QUAD // 2) + pair
-                    copy = nc.scalar.copy
-                    if kind == "x" and b == 0 and a == UNIT_BANKS - 1:
-                        copy = nc.vector.tensor_copy
-                    copy(
+                    nc.scalar.copy(
                         out=words[:, q, 2 * pair : 2 * pair + 2, :, :],
-                        in_=banks[n][a][:].rearrange("w s u c -> w s c u"),
+                        in_=banks[n][q * (QUAD // 2) + pair][:].rearrange("w s u c -> w s c u"),
                     )
             groupeds[n] = grouped
+
+        def sum_pairs(n):
+            sum2 = work.tile([P, UNIT_PASSES * 2, PLANE], F32, name="sum2", bufs=3)
+            for q in range(UNIT_PASSES):
+                for pair in range(QUAD // 2):
+                    a = q * (QUAD // 2) + pair
+                    rows = banks[n][a][:].bitcast(BF16).rearrange("w s u (c e) -> w s c u e", e=2)
+                    nc.vector.tensor_tensor(
+                        out=sum2[:, a, :].rearrange("w (c u e) -> w c u e", u=2, e=2),
+                        in0=rows[:, 1, :, :, :],
+                        in1=groupeds[n][:, q, 2 * pair, :].rearrange("w (c u e) -> w c u e", u=2, e=2),
+                        op=ADD,
+                    )
+            sums2[n] = sum2
 
         def quantise(values, name):
             width = values.shape[1] // PACK
@@ -129,9 +142,7 @@ def tile_contractexpand_pa_k_kernel(tc, inputs_c_e, Ws, bs, out):
             passes = slice(h * UNIT_PASSES, (h + 1) * UNIT_PASSES)
             grouped = groupeds[n]
 
-            pairs = grouped[:].rearrange("w q (m two) v -> w (q m) two v", two=2)
-            sum2 = work.tile([P, UNIT_PASSES * 2, PLANE], F32, name="sum2")
-            nc.vector.tensor_tensor(out=sum2[:], in0=pairs[:, :, 0, :], in1=pairs[:, :, 1, :], op=ADD)
+            sum2 = sums2[n]
             halves = sum2[:].rearrange("w (q m) v -> w q m v", m=2)
             if b == 0:
                 sum4 = run12[:, passes, :]
@@ -143,28 +154,34 @@ def tile_contractexpand_pa_k_kernel(tc, inputs_c_e, Ws, bs, out):
             sum2_bf = work.tile([P, UNIT_PASSES * 2, PLANE], BF16, name="sum2_bf", align_bytes=64)
             nc.scalar.copy(out=sum2_bf[:], in_=sum2[:])
             sum4_bf = work.tile([P, UNIT_PASSES, PLANE], BF16, name="sum4_bf", align_bytes=64)
-            nc.scalar.copy(out=sum4_bf[:], in_=sum4)
+            if b == 0:
+                nc.vector.tensor_copy(out=sum4_bf[:], in_=sum4)
+            else:
+                nc.scalar.copy(out=sum4_bf[:], in_=sum4)
 
             if b == 1:
-                nc.vector.tensor_tensor(out=run12[:, passes, :], in0=run12[:, passes, :], in1=sum4, op=ADD)
+                nc.gpsimd.tensor_tensor(out=run12[:, passes, :], in0=run12[:, passes, :], in1=sum4, op=ADD)
             if b == N_BLOCKS - 1:
                 sum12_bf = work.tile([P, UNIT_PASSES, PLANE], BF16, name="sum12_bf", align_bytes=64)
-                nc.vector.tensor_tensor(out=sum12_bf[:], in0=run12[:, passes, :], in1=sum4, op=ADD)
+                nc.gpsimd.tensor_tensor(out=sum12_bf[:], in0=run12[:, passes, :], in1=sum4, op=ADD)
+                sums12[n] = sum12_bf
 
             operands[n] = [
                 quantise(grouped[:].rearrange("w q s v -> w (q s v)"), "x"),
                 quantise(sum2_bf[:].rearrange("w a v -> w (a v)"), "sum2"),
                 quantise(sum4_bf[:].rearrange("w q v -> w (q v)"), "sum4"),
             ]
-            if b == N_BLOCKS - 1:
-                operands[n].append(quantise(sum12_bf[:].rearrange("w q v -> w (q v)"), "sum12"))
+
+        def quantise_sum12(n):
+            operands[n].append(quantise(sums12[n][:].rearrange("w q v -> w (q v)"), "sum12"))
 
         def multiply(n):
             b, h = units[n][1], units[n][2]
             for i in range(len(operands[n])):
-                if h == 0:
-                    planes = max(QUAD // SCALES[i], 1)
-                    accs[i] = acc_pool.tile([P, planes * P], F32, name="acc%d" % i, tag="bank%d" % i)
+                if h == 0 and SCALES[i] <= QUAD:
+                    accs[i] = acc_pool.tile([P, QUAD // SCALES[i] * P], F32, name="acc%d" % i, tag="bank%d" % i)
+                if h == 0 and SCALES[i] > QUAD:
+                    accs[i] = flip_pool.tile([P, P], F32, name="acc%d" % i, tag="bank")
                 codes, scales = operands[n][i]
                 width = codes.shape[1] // UNIT_PASSES
                 for q in range(UNIT_PASSES):
@@ -198,7 +215,7 @@ def tile_contractexpand_pa_k_kernel(tc, inputs_c_e, Ws, bs, out):
                 relus.append(relu)
             for i in range(n_scales):
                 planes = accs[i].shape[1] // P
-                back = acc_pool.tile([P, planes, P], F32, name="back%d" % i, tag="bank%d" % i)
+                back = flip_pool.tile([P, planes, P], F32, name="back%d" % i, tag="bank")
                 for m in range(planes):
                     nc.tensor.transpose(back[:, m, :], relus[i][:, m, :], identity[:])
                 backs.append(back)
@@ -214,23 +231,27 @@ def tile_contractexpand_pa_k_kernel(tc, inputs_c_e, Ws, bs, out):
                         out=out_rows[:, i, rows, :], in_=result[:, m : m + 1, :].to_broadcast([P, r, P])
                     )
 
-        with tc.manual_schedule():
-            for n in range(3):
-                load(n)
-            transpose(0)
-            copy_out(0)
-            transpose(1)
-            for n in range(len(units) + 1):
-                if n + 3 < len(units):
-                    load(n + 3)
-                if n + 1 < len(units):
-                    copy_out(n + 1)
-                if n + 2 < len(units):
-                    transpose(n + 2)
-                if n < len(units):
-                    if units[n][0] == "w":
-                        quantise_weights(n)
-                    else:
-                        sum_and_quantise(n)
-                if n >= 1 and units[n - 1][0] == "x":
-                    multiply(n - 1)
+        for n in range(3):
+            load(n)
+        transpose(0)
+        copy_out(0)
+        sum_pairs(0)
+        transpose(1)
+        for n in range(len(units) + 1):
+            if n + 3 < len(units):
+                load(n + 3)
+            if n + 1 < len(units):
+                copy_out(n + 1)
+                if units[n + 1][0] == "x":
+                    sum_pairs(n + 1)
+            if n + 2 < len(units):
+                transpose(n + 2)
+            if n < len(units):
+                if units[n][0] == "w":
+                    quantise_weights(n)
+                else:
+                    sum_and_quantise(n)
+            if n >= 1 and units[n - 1][0] == "x":
+                if units[n - 1][1] == N_BLOCKS - 1:
+                    quantise_sum12(n - 1)
+                multiply(n - 1)

@@ -8,6 +8,7 @@ U8 = mybir.dt.uint8
 FP8X4 = mybir.dt.float8_e4m3fn_x4
 ADD = mybir.AluOpType.add
 RELU = mybir.ActivationFunctionType.Relu
+AXIS_X = mybir.AxisListType.X
 
 P = 128
 N_ROWS = 1536
@@ -16,21 +17,27 @@ SCALES = (1, 2, 4, 12)
 GROUP = 12
 QUAD = 4
 N_BLOCKS = GROUP // QUAD
+TILES = 4
+QUADS = P // QUAD
 PACK = 4
 K_PASS = P * PACK
 N_PASSES = D // K_PASS
 UNIT_PASSES = 2
 N_UNITS = N_PASSES // UNIT_PASSES
+K_UNIT = K_PASS * UNIT_PASSES
 PLANE = P * PACK
 FLIP_BANKS = 5
 
 FLOPS = 2 * sum(N_ROWS // r for r in SCALES) * D * P
 
 
+def sums_on_tensor(b):
+    return b > 0
+
+
 def tile_contractexpand_pa_k_kernel(tc, inputs_c_e, Ws, bs, out):
     nc = tc.nc
-    x_rows = inputs_c_e.rearrange("(c j) k -> c j k", j=GROUP)
-    w_rows = Ws.rearrange("i o k -> o i k")
+    x_rows = inputs_c_e.rearrange("(t cc b i) k -> b i cc t k", t=TILES, cc=QUADS, b=N_BLOCKS)
     out_rows = out.rearrange("(i c j) o -> c i j o", i=len(SCALES), j=GROUP)
 
     units = []
@@ -41,14 +48,22 @@ def tile_contractexpand_pa_k_kernel(tc, inputs_c_e, Ws, bs, out):
         for h in range(N_UNITS):
             units.append(("x", b, h))
 
-    with tc.tile_pool(name="keep", bufs=1) as keep, tc.tile_pool(name="raw", bufs=3) as raw_pool, tc.tile_pool(
+    with tc.tile_pool(name="keep", bufs=1) as keep, tc.tile_pool(name="raw", bufs=4) as raw_pool, tc.tile_pool(
         name="work", bufs=2
     ) as work, tc.psum_pool(name="flip", bufs=FLIP_BANKS) as flip_pool, tc.psum_pool(name="acc", bufs=1) as acc_pool:
         identity = keep.tile([P, P], F32, name="identity")
         make_identity(nc, identity[:])
+        adder_wide = keep.tile([P, QUADS], F32, name="adder_wide")
+        nc.vector.tensor_reduce(
+            out=adder_wide[:], in_=identity[:].rearrange("p (cc i) -> p cc i", i=QUAD), axis=AXIS_X, op=ADD
+        )
+        adder = keep.tile([P, QUADS], BF16, name="adder")
+        nc.vector.tensor_copy(out=adder[:], in_=adder_wide[:])
 
         w_codes = keep.tile([P, N_PASSES, len(SCALES), P], U32, name="w_codes", align_bytes=64)
         w_scales = keep.tile([P, N_PASSES, len(SCALES), P], U8, name="w_scales", align_bytes=64)
+        codes12 = keep.tile([P, N_PASSES, P], U32, name="codes12", align_bytes=64)
+        scales12 = keep.tile([P, N_PASSES, P], U8, name="scales12", align_bytes=64)
         run12 = keep.tile([P, N_PASSES, PLANE], F32, name="run12")
 
         bias_rows = keep.tile([P, P], BF16, name="bias_rows")
@@ -64,62 +79,97 @@ def tile_contractexpand_pa_k_kernel(tc, inputs_c_e, Ws, bs, out):
         raws = {}
         banks = {}
         groupeds = {}
-        sums2 = {}
+        quad_banks = {}
+        sums4 = {}
         sums12 = {}
         operands = {}
         accs = {}
 
         def load(n):
             kind, b, h = units[n]
-            source = w_rows if kind == "w" else x_rows
-            raw = raw_pool.tile([P, UNIT_PASSES, QUAD, K_PASS], BF16, name="raw")
-            for q in range(UNIT_PASSES):
-                g = h * UNIT_PASSES + q
-                for pair in range(QUAD // 2):
-                    first = b * QUAD + 2 * pair
-                    nc.sync.dma_start(
-                        out=raw[:, q, 2 * pair : 2 * pair + 2, :],
-                        in_=source[:, first : first + 2, g * K_PASS : (g + 1) * K_PASS],
-                    )
+            ks = slice(h * K_UNIT, (h + 1) * K_UNIT)
+            raw = raw_pool.tile([P, TILES, K_UNIT], BF16, name="raw")
+            for i in range(QUAD):
+                if kind == "w":
+                    nc.sync.dma_start(out=raw[:, i, :], in_=Ws[i, :, ks])
+                else:
+                    nc.sync.dma_start(out=raw[i:P:QUAD, :, :], in_=x_rows[b, i, :, :, ks])
             raws[n] = raw
 
         def transpose(n):
             words = raws[n][:].bitcast(F32)
             banks[n] = []
             for q in range(UNIT_PASSES):
-                for pair in range(QUAD // 2):
+                for pair in range(TILES // 2):
                     bank = flip_pool.tile([P, 2, 2, P], F32, name="bank")
                     for s in range(2):
                         for u in range(2):
+                            first = (2 * q + u) * P
                             nc.tensor.transpose(
-                                bank[:, s, u, :], words[:, q, 2 * pair + s, u * P : (u + 1) * P], identity[:]
+                                bank[:, u, s, :], words[:, 2 * pair + s, first : first + P], identity[:]
                             )
                     banks[n].append(bank)
 
         def copy_out(n):
+            kind = units[n][0]
             grouped = work.tile([P, UNIT_PASSES, QUAD, PLANE], BF16, name="grouped", align_bytes=64, bufs=3)
-            words = grouped[:].bitcast(F32).rearrange("w q s (c u) -> w q s c u", u=2)
+            words = grouped[:].bitcast(F32).rearrange("w q i (c u) -> w q i c u", u=2)
             for q in range(UNIT_PASSES):
-                for pair in range(QUAD // 2):
-                    nc.scalar.copy(
-                        out=words[:, q, 2 * pair : 2 * pair + 2, :, :],
-                        in_=banks[n][q * (QUAD // 2) + pair][:].rearrange("w s u c -> w s c u"),
-                    )
+                for pair in range(TILES // 2):
+                    bank = banks[n][q * (TILES // 2) + pair]
+                    if kind == "w":
+                        nc.scalar.copy(
+                            out=words[:, q, 2 * pair : 2 * pair + 2, :, :],
+                            in_=bank[:].rearrange("w u s o -> w s o u"),
+                        )
+                    else:
+                        half = P // 2
+                        nc.scalar.copy(
+                            out=words[:, q, :, pair * half : (pair + 1) * half, :],
+                            in_=bank[:].rearrange("w u s (cc i) -> w i (s cc) u", i=QUAD),
+                        )
             groupeds[n] = grouped
 
-        def sum_pairs(n):
-            sum2 = work.tile([P, UNIT_PASSES * 2, PLANE], F32, name="sum2", bufs=3)
+        def add_quads(n):
+            if not sums_on_tensor(units[n][1]):
+                return
+            raw = raws[n]
+            quad_banks[n] = []
             for q in range(UNIT_PASSES):
-                for pair in range(QUAD // 2):
-                    a = q * (QUAD // 2) + pair
-                    rows = banks[n][a][:].bitcast(BF16).rearrange("w s u (c e) -> w s c u e", e=2)
+                bank = flip_pool.tile([P, PACK, P], F32, name="quad_bank", tag="bank")
+                for t in range(TILES):
+                    for u in range(2):
+                        for e in range(2):
+                            first = q * K_PASS + u * 2 * P + e
+                            nc.tensor.matmul(
+                                bank[:, 2 * u + e, t * QUADS : (t + 1) * QUADS],
+                                lhsT=raw[:, t, first : (2 * q + u + 1) * 2 * P : 2],
+                                rhs=adder[:],
+                                start=True,
+                                stop=True,
+                            )
+                quad_banks[n].append(bank)
+
+        def take_quads(n):
+            b, h = units[n][1], units[n][2]
+            if not sums_on_tensor(b):
+                return
+            sum4_bf = work.tile([P, UNIT_PASSES, PLANE], BF16, name="sum4_bf", align_bytes=64)
+            sums4[n] = sum4_bf
+            if b == N_BLOCKS - 1:
+                sum12_bf = work.tile([P, UNIT_PASSES, PLANE], BF16, name="sum12_bf", align_bytes=64)
+                sums12[n] = sum12_bf
+            for q in range(UNIT_PASSES):
+                g = h * UNIT_PASSES + q
+                values = quad_banks[n][q][:].rearrange("w v c -> w c v")
+                nc.scalar.copy(out=sum4_bf[:, q, :].rearrange("w (c v) -> w c v", v=PACK), in_=values)
+                carry = run12[:, g, :].rearrange("w (c v) -> w c v", v=PACK)
+                if b == N_BLOCKS - 1:
                     nc.vector.tensor_tensor(
-                        out=sum2[:, a, :].rearrange("w (c u e) -> w c u e", u=2, e=2),
-                        in0=rows[:, 1, :, :, :],
-                        in1=groupeds[n][:, q, 2 * pair, :].rearrange("w (c u e) -> w c u e", u=2, e=2),
-                        op=ADD,
+                        out=sum12_bf[:, q, :].rearrange("w (c v) -> w c v", v=PACK), in0=values, in1=carry, op=ADD
                     )
-            sums2[n] = sum2
+                else:
+                    nc.vector.tensor_tensor(out=carry, in0=values, in1=carry, op=ADD)
 
         def quantise(values, name):
             width = values.shape[1] // PACK
@@ -141,47 +191,39 @@ def tile_contractexpand_pa_k_kernel(tc, inputs_c_e, Ws, bs, out):
             b, h = units[n][1], units[n][2]
             passes = slice(h * UNIT_PASSES, (h + 1) * UNIT_PASSES)
             grouped = groupeds[n]
-
-            sum2 = sums2[n]
-            halves = sum2[:].rearrange("w (q m) v -> w q m v", m=2)
-            if b == 0:
-                sum4 = run12[:, passes, :]
-            else:
-                sum4_tile = work.tile([P, UNIT_PASSES, PLANE], F32, name="sum4")
-                sum4 = sum4_tile[:]
-            nc.vector.tensor_tensor(out=sum4, in0=halves[:, :, 0, :], in1=halves[:, :, 1, :], op=ADD)
+            rows = grouped[:].rearrange("w q (m s) v -> w (q m) s v", s=2)
 
             sum2_bf = work.tile([P, UNIT_PASSES * 2, PLANE], BF16, name="sum2_bf", align_bytes=64)
-            nc.scalar.copy(out=sum2_bf[:], in_=sum2[:])
-            sum4_bf = work.tile([P, UNIT_PASSES, PLANE], BF16, name="sum4_bf", align_bytes=64)
-            if b == 0:
-                nc.vector.tensor_copy(out=sum4_bf[:], in_=sum4)
-            else:
-                nc.scalar.copy(out=sum4_bf[:], in_=sum4)
+            nc.vector.tensor_tensor(out=sum2_bf[:], in0=rows[:, :, 0, :], in1=rows[:, :, 1, :], op=ADD)
 
-            if b == 1:
-                nc.gpsimd.tensor_tensor(out=run12[:, passes, :], in0=run12[:, passes, :], in1=sum4, op=ADD)
-            if b == N_BLOCKS - 1:
-                sum12_bf = work.tile([P, UNIT_PASSES, PLANE], BF16, name="sum12_bf", align_bytes=64)
-                nc.gpsimd.tensor_tensor(out=sum12_bf[:], in0=run12[:, passes, :], in1=sum4, op=ADD)
-                sums12[n] = sum12_bf
+            if not sums_on_tensor(b):
+                sum2 = work.tile([P, UNIT_PASSES * 2, PLANE], F32, name="sum2")
+                nc.vector.tensor_tensor(out=sum2[:], in0=rows[:, :, 0, :], in1=rows[:, :, 1, :], op=ADD)
+                halves = sum2[:].rearrange("w (q m) v -> w q m v", m=2)
+                nc.vector.tensor_tensor(
+                    out=run12[:, passes, :], in0=halves[:, :, 0, :], in1=halves[:, :, 1, :], op=ADD
+                )
+                sum4_bf = work.tile([P, UNIT_PASSES, PLANE], BF16, name="sum4_bf", align_bytes=64)
+                nc.scalar.copy(out=sum4_bf[:], in_=run12[:, passes, :])
+                sums4[n] = sum4_bf
 
             operands[n] = [
                 quantise(grouped[:].rearrange("w q s v -> w (q s v)"), "x"),
                 quantise(sum2_bf[:].rearrange("w a v -> w (a v)"), "sum2"),
-                quantise(sum4_bf[:].rearrange("w q v -> w (q v)"), "sum4"),
+                quantise(sums4[n][:].rearrange("w q v -> w (q v)"), "sum4"),
             ]
-
-        def quantise_sum12(n):
-            operands[n].append(quantise(sums12[n][:].rearrange("w q v -> w (q v)"), "sum12"))
+            if b == N_BLOCKS - 1:
+                nc.vector.quantize_mx(
+                    out=codes12[:, passes, :].rearrange("w g c -> w (g c)").bitcast(FP8X4),
+                    scales=scales12[:, passes, :].rearrange("w g c -> w (g c)"),
+                    in_=sums12[n][:].rearrange("w q v -> w (q v)"),
+                )
 
         def multiply(n):
             b, h = units[n][1], units[n][2]
             for i in range(len(operands[n])):
-                if h == 0 and SCALES[i] <= QUAD:
+                if h == 0:
                     accs[i] = acc_pool.tile([P, QUAD // SCALES[i] * P], F32, name="acc%d" % i, tag="bank%d" % i)
-                if h == 0 and SCALES[i] > QUAD:
-                    accs[i] = flip_pool.tile([P, P], F32, name="acc%d" % i, tag="bank")
                 codes, scales = operands[n][i]
                 width = codes.shape[1] // UNIT_PASSES
                 for q in range(UNIT_PASSES):
@@ -197,7 +239,21 @@ def tile_contractexpand_pa_k_kernel(tc, inputs_c_e, Ws, bs, out):
                         stop=(g == N_PASSES - 1),
                     )
             if h == N_UNITS - 1:
-                finish(b, len(operands[n]))
+                n_scales = len(operands[n])
+                if b == N_BLOCKS - 1:
+                    accs[n_scales] = flip_pool.tile([P, P], F32, name="acc12", tag="bank")
+                    for g in range(N_PASSES):
+                        nc.tensor.matmul_mx(
+                            out=accs[n_scales][:],
+                            lhsT=w_codes[:, g, n_scales, :].bitcast(FP8X4),
+                            lhsT_scale=w_scales[:, g, n_scales, :],
+                            rhs=codes12[:, g, :].bitcast(FP8X4),
+                            rhs_scale=scales12[:, g, :],
+                            start=(g == 0),
+                            stop=(g == N_PASSES - 1),
+                        )
+                    n_scales += 1
+                finish(b, n_scales)
 
         def finish(b, n_scales):
             relus = []
@@ -235,7 +291,8 @@ def tile_contractexpand_pa_k_kernel(tc, inputs_c_e, Ws, bs, out):
             load(n)
         transpose(0)
         copy_out(0)
-        sum_pairs(0)
+        add_quads(0)
+        take_quads(0)
         transpose(1)
         for n in range(len(units) + 1):
             if n + 3 < len(units):
@@ -243,7 +300,8 @@ def tile_contractexpand_pa_k_kernel(tc, inputs_c_e, Ws, bs, out):
             if n + 1 < len(units):
                 copy_out(n + 1)
                 if units[n + 1][0] == "x":
-                    sum_pairs(n + 1)
+                    add_quads(n + 1)
+                    take_quads(n + 1)
             if n + 2 < len(units):
                 transpose(n + 2)
             if n < len(units):
@@ -252,6 +310,4 @@ def tile_contractexpand_pa_k_kernel(tc, inputs_c_e, Ws, bs, out):
                 else:
                     sum_and_quantise(n)
             if n >= 1 and units[n - 1][0] == "x":
-                if units[n - 1][1] == N_BLOCKS - 1:
-                    quantise_sum12(n - 1)
                 multiply(n - 1)

@@ -42,13 +42,13 @@ def tile_contractexpand_pa_k_kernel(tc, inputs_c_e, Ws, bs, out):
 
     units = []
     for h in range(N_UNITS):
-        units.append(("x", 0, h))
         units.append(("w", 0, h))
+        units.append(("x", 0, h))
     for b in range(1, N_BLOCKS):
         for h in range(N_UNITS):
             units.append(("x", b, h))
 
-    with tc.tile_pool(name="keep", bufs=1) as keep, tc.tile_pool(name="raw", bufs=4) as raw_pool, tc.tile_pool(
+    with tc.tile_pool(name="keep", bufs=1) as keep, tc.tile_pool(name="raw", bufs=5) as raw_pool, tc.tile_pool(
         name="work", bufs=2
     ) as work, tc.psum_pool(name="flip", bufs=FLIP_BANKS) as flip_pool, tc.psum_pool(name="acc", bufs=1) as acc_pool:
         identity = keep.tile([P, P], F32, name="identity")
@@ -80,10 +80,14 @@ def tile_contractexpand_pa_k_kernel(tc, inputs_c_e, Ws, bs, out):
         banks = {}
         groupeds = {}
         quad_banks = {}
+        sums2 = {}
         sums4 = {}
         sums12 = {}
         operands = {}
         accs = {}
+        relus = {}
+        backs = {}
+        results = {}
 
         def load(n):
             kind, b, h = units[n]
@@ -150,31 +154,37 @@ def tile_contractexpand_pa_k_kernel(tc, inputs_c_e, Ws, bs, out):
                             )
                 quad_banks[n].append(bank)
 
-        def take_quads(n):
-            b, h = units[n][1], units[n][2]
-            if not sums_on_tensor(b):
+        def round_quads(n):
+            if not sums_on_tensor(units[n][1]):
                 return
             sum4_bf = work.tile([P, UNIT_PASSES, PLANE], BF16, name="sum4_bf", align_bytes=64)
             sums4[n] = sum4_bf
+            for q in range(UNIT_PASSES):
+                nc.scalar.copy(
+                    out=sum4_bf[:, q, :].rearrange("w (c v) -> w c v", v=PACK),
+                    in_=quad_banks[n][q][:].rearrange("w v c -> w c v"),
+                )
+
+        def carry_quads(n):
+            b, h = units[n][1], units[n][2]
+            if not sums_on_tensor(b):
+                return
             if b == N_BLOCKS - 1:
                 sum12_bf = work.tile([P, UNIT_PASSES, PLANE], BF16, name="sum12_bf", align_bytes=64)
                 sums12[n] = sum12_bf
             for q in range(UNIT_PASSES):
-                g = h * UNIT_PASSES + q
-                values = quad_banks[n][q][:].rearrange("w v c -> w c v")
-                nc.scalar.copy(out=sum4_bf[:, q, :].rearrange("w (c v) -> w c v", v=PACK), in_=values)
-                carry = run12[:, g, :].rearrange("w (c v) -> w c v", v=PACK)
+                carry = run12[:, h * UNIT_PASSES + q, :].rearrange("w (c v) -> w c v", v=PACK)
+                target = carry
                 if b == N_BLOCKS - 1:
-                    nc.vector.tensor_tensor(
-                        out=sum12_bf[:, q, :].rearrange("w (c v) -> w c v", v=PACK), in0=values, in1=carry, op=ADD
-                    )
-                else:
-                    nc.vector.tensor_tensor(out=carry, in0=values, in1=carry, op=ADD)
+                    target = sum12_bf[:, q, :].rearrange("w (c v) -> w c v", v=PACK)
+                nc.vector.tensor_tensor(
+                    out=target, in0=quad_banks[n][q][:].rearrange("w v c -> w c v"), in1=carry, op=ADD
+                )
 
         def quantise(values, name):
             width = values.shape[1] // PACK
-            codes = work.tile([P, width], U32, name=name + "_codes", align_bytes=64)
-            scales = work.tile([P, width], U8, name=name + "_scales", align_bytes=64)
+            codes = work.tile([P, width], U32, name=name + "_codes", align_bytes=64, bufs=3)
+            scales = work.tile([P, width], U8, name=name + "_scales", align_bytes=64, bufs=3)
             nc.vector.quantize_mx(out=codes[:].bitcast(FP8X4), scales=scales[:], in_=values)
             return codes, scales
 
@@ -187,127 +197,148 @@ def tile_contractexpand_pa_k_kernel(tc, inputs_c_e, Ws, bs, out):
                 in_=groupeds[n][:].rearrange("w q s v -> w (q s v)"),
             )
 
-        def sum_and_quantise(n):
+        def add_pairs(n):
             b, h = units[n][1], units[n][2]
             passes = slice(h * UNIT_PASSES, (h + 1) * UNIT_PASSES)
-            grouped = groupeds[n]
-            rows = grouped[:].rearrange("w q (m s) v -> w (q m) s v", s=2)
-
+            rows = groupeds[n][:].rearrange("w q (m s) v -> w (q m) s v", s=2)
             sum2_bf = work.tile([P, UNIT_PASSES * 2, PLANE], BF16, name="sum2_bf", align_bytes=64)
-            nc.vector.tensor_tensor(out=sum2_bf[:], in0=rows[:, :, 0, :], in1=rows[:, :, 1, :], op=ADD)
+            sums2[n] = sum2_bf
+            if sums_on_tensor(b):
+                nc.vector.tensor_tensor(out=sum2_bf[:], in0=rows[:, :, 0, :], in1=rows[:, :, 1, :], op=ADD)
+                return
+            sum2 = work.tile([P, UNIT_PASSES * 2, PLANE], F32, name="sum2")
+            nc.vector.tensor_tensor(out=sum2[:], in0=rows[:, :, 0, :], in1=rows[:, :, 1, :], op=ADD)
+            nc.scalar.copy(out=sum2_bf[:, 2:4, :], in_=sum2[:, 2:4, :])
+            nc.vector.tensor_tensor(out=sum2_bf[:, 0:2, :], in0=rows[:, 0:2, 0, :], in1=rows[:, 0:2, 1, :], op=ADD)
+            halves = sum2[:].rearrange("w (q m) v -> w q m v", m=2)
+            nc.vector.tensor_tensor(out=run12[:, passes, :], in0=halves[:, :, 0, :], in1=halves[:, :, 1, :], op=ADD)
+            sum4_bf = work.tile([P, UNIT_PASSES, PLANE], BF16, name="sum4_bf", align_bytes=64)
+            nc.scalar.copy(out=sum4_bf[:], in_=run12[:, passes, :])
+            sums4[n] = sum4_bf
 
-            if not sums_on_tensor(b):
-                sum2 = work.tile([P, UNIT_PASSES * 2, PLANE], F32, name="sum2")
-                nc.vector.tensor_tensor(out=sum2[:], in0=rows[:, :, 0, :], in1=rows[:, :, 1, :], op=ADD)
-                halves = sum2[:].rearrange("w (q m) v -> w q m v", m=2)
-                nc.vector.tensor_tensor(
-                    out=run12[:, passes, :], in0=halves[:, :, 0, :], in1=halves[:, :, 1, :], op=ADD
-                )
-                sum4_bf = work.tile([P, UNIT_PASSES, PLANE], BF16, name="sum4_bf", align_bytes=64)
-                nc.scalar.copy(out=sum4_bf[:], in_=run12[:, passes, :])
-                sums4[n] = sum4_bf
+        def quantise_rows(n):
+            operands[n] = {0: quantise(groupeds[n][:].rearrange("w q s v -> w (q s v)"), "x")}
 
-            operands[n] = [
-                quantise(grouped[:].rearrange("w q s v -> w (q s v)"), "x"),
-                quantise(sum2_bf[:].rearrange("w a v -> w (a v)"), "sum2"),
-                quantise(sums4[n][:].rearrange("w q v -> w (q v)"), "sum4"),
-            ]
+        def quantise_sums(n):
+            b, h = units[n][1], units[n][2]
+            operands[n][2] = quantise(sums4[n][:].rearrange("w q v -> w (q v)"), "sum4")
             if b == N_BLOCKS - 1:
+                passes = slice(h * UNIT_PASSES, (h + 1) * UNIT_PASSES)
                 nc.vector.quantize_mx(
                     out=codes12[:, passes, :].rearrange("w g c -> w (g c)").bitcast(FP8X4),
                     scales=scales12[:, passes, :].rearrange("w g c -> w (g c)"),
                     in_=sums12[n][:].rearrange("w q v -> w (q v)"),
                 )
+            operands[n][1] = quantise(sums2[n][:].rearrange("w a v -> w (a v)"), "sum2")
 
         def multiply(n):
-            b, h = units[n][1], units[n][2]
+            h = units[n][2]
             for i in range(len(operands[n])):
                 if h == 0:
                     accs[i] = acc_pool.tile([P, QUAD // SCALES[i] * P], F32, name="acc%d" % i, tag="bank%d" % i)
                 codes, scales = operands[n][i]
                 width = codes.shape[1] // UNIT_PASSES
                 for q in range(UNIT_PASSES):
-                    g = h * UNIT_PASSES + q
                     cols = slice(q * width, (q + 1) * width)
-                    nc.tensor.matmul_mx(
-                        out=accs[i][:],
-                        lhsT=w_codes[:, g, i, :].bitcast(FP8X4),
-                        lhsT_scale=w_scales[:, g, i, :],
-                        rhs=codes[:, cols].bitcast(FP8X4),
-                        rhs_scale=scales[:, cols],
-                        start=(g == 0),
-                        stop=(g == N_PASSES - 1),
-                    )
-            if h == N_UNITS - 1:
-                n_scales = len(operands[n])
-                if b == N_BLOCKS - 1:
-                    accs[n_scales] = flip_pool.tile([P, P], F32, name="acc12", tag="bank")
-                    for g in range(N_PASSES):
-                        nc.tensor.matmul_mx(
-                            out=accs[n_scales][:],
-                            lhsT=w_codes[:, g, n_scales, :].bitcast(FP8X4),
-                            lhsT_scale=w_scales[:, g, n_scales, :],
-                            rhs=codes12[:, g, :].bitcast(FP8X4),
-                            rhs_scale=scales12[:, g, :],
-                            start=(g == 0),
-                            stop=(g == N_PASSES - 1),
-                        )
-                    n_scales += 1
-                finish(b, n_scales)
+                    multiply_pass(i, h * UNIT_PASSES + q, codes[:, cols], scales[:, cols])
 
-        def finish(b, n_scales):
-            relus = []
-            backs = []
-            for i in range(n_scales):
-                planes = accs[i].shape[1] // P
-                relu = work.tile([P, planes, P], F32, name="relu%d" % i)
-                nc.scalar.activation(
-                    out=relu[:].rearrange("o m c -> o (m c)"),
-                    in_=accs[i][:],
-                    func=RELU,
-                    bias=bias[:, i : i + 1],
-                    scale=1.0,
+        def multiply_pass(i, g, codes, scales):
+            nc.tensor.matmul_mx(
+                out=accs[i][:],
+                lhsT=w_codes[:, g, i, :].bitcast(FP8X4),
+                lhsT_scale=w_scales[:, g, i, :],
+                rhs=codes.bitcast(FP8X4),
+                rhs_scale=scales,
+                start=(g == 0),
+                stop=(g == N_PASSES - 1),
+            )
+
+        def multiply12(first, last):
+            if first == 0:
+                accs[3] = flip_pool.tile([P, P], F32, name="acc12", tag="bank")
+            for g in range(first, last):
+                multiply_pass(3, g, codes12[:, g, :], scales12[:, g, :])
+
+        def apply_relu(i):
+            planes = accs[i].shape[1] // P
+            relu = work.tile([P, planes, P], F32, name="relu%d" % i)
+            nc.scalar.activation(
+                out=relu[:].rearrange("o m c -> o (m c)"),
+                in_=accs[i][:],
+                func=RELU,
+                bias=bias[:, i : i + 1],
+                scale=1.0,
+            )
+            relus[i] = relu
+
+        def turn_back(i):
+            planes = relus[i].shape[1]
+            back = flip_pool.tile([P, planes, P], F32, name="back%d" % i, tag="bank")
+            for m in range(planes):
+                nc.tensor.transpose(back[:, m, :], relus[i][:, m, :], identity[:])
+            backs[i] = back
+
+        def divide(i):
+            planes = relus[i].shape[1]
+            result = work.tile([P, planes, P], F32, name="result%d" % i)
+            nc.scalar.mul(out=result[:], in_=backs[i][:], mul=1.0 / SCALES[i])
+            results[i] = result
+
+        def store(b, i):
+            r = SCALES[i]
+            first_row = b * QUAD if r <= QUAD else 0
+            for m in range(results[i].shape[1]):
+                rows = slice(first_row + m * r, first_row + (m + 1) * r)
+                nc.sync.dma_start(
+                    out=out_rows[:, i, rows, :], in_=results[i][:, m : m + 1, :].to_broadcast([P, r, P])
                 )
-                relus.append(relu)
-            for i in range(n_scales):
-                planes = accs[i].shape[1] // P
-                back = flip_pool.tile([P, planes, P], F32, name="back%d" % i, tag="bank")
-                for m in range(planes):
-                    nc.tensor.transpose(back[:, m, :], relus[i][:, m, :], identity[:])
-                backs.append(back)
-            for i in range(n_scales):
-                r = SCALES[i]
-                planes = accs[i].shape[1] // P
-                first_row = b * QUAD if r <= QUAD else 0
-                result = work.tile([P, planes, P], F32, name="result%d" % i)
-                nc.scalar.mul(out=result[:], in_=backs[i][:], mul=1.0 / r)
-                for m in range(planes):
-                    rows = slice(first_row + m * r, first_row + (m + 1) * r)
-                    nc.sync.dma_start(
-                        out=out_rows[:, i, rows, :], in_=result[:, m : m + 1, :].to_broadcast([P, r, P])
-                    )
 
-        for n in range(3):
-            load(n)
-        transpose(0)
-        copy_out(0)
-        add_quads(0)
-        take_quads(0)
-        transpose(1)
-        for n in range(len(units) + 1):
-            if n + 3 < len(units):
-                load(n + 3)
-            if n + 1 < len(units):
-                copy_out(n + 1)
-                if units[n + 1][0] == "x":
-                    add_quads(n + 1)
-                    take_quads(n + 1)
-            if n + 2 < len(units):
-                transpose(n + 2)
-            if n < len(units):
-                if units[n][0] == "w":
+        last = len(units) - 1
+        with tc.manual_schedule():
+            for n in range(4):
+                load(n)
+            for n in range(-1, len(units) + 2):
+                if n >= 0 and n + 4 <= last:
+                    load(n + 4)
+                done = n - 3
+                finished = 0 <= done <= last and units[done][0] == "x" and units[done][2] == N_UNITS - 1
+                if finished:
+                    for i in range(3):
+                        apply_relu(i)
+                if n + 1 <= last:
+                    transpose(n + 1)
+                    copy_out(n + 1)
+                    if units[n + 1][0] == "x":
+                        add_quads(n + 1)
+                        round_quads(n + 1)
+                if 0 <= n <= last and units[n][0] == "x":
+                    add_pairs(n)
+                    quantise_rows(n)
+                if 0 <= n <= last and units[n][0] == "w":
                     quantise_weights(n)
-                else:
-                    sum_and_quantise(n)
-            if n >= 1 and units[n - 1][0] == "x":
-                multiply(n - 1)
+                if 0 <= n - 1 <= last and units[n - 1][0] == "x" and not sums_on_tensor(units[n - 1][1]):
+                    quantise_sums(n - 1)
+                if 0 <= n <= last and units[n][0] == "x" and sums_on_tensor(units[n][1]):
+                    quantise_sums(n)
+                if n + 1 <= last and units[n + 1][0] == "x":
+                    carry_quads(n + 1)
+                if n == last:
+                    multiply12(0, N_PASSES - UNIT_PASSES)
+                if 0 <= n - 2 <= last and units[n - 2][0] == "x":
+                    multiply(n - 2)
+                if finished:
+                    for i in range(3):
+                        turn_back(i)
+                    for i in range(3):
+                        divide(i)
+                    for i in range(3):
+                        store(units[done][1], i)
+            multiply12(N_PASSES - UNIT_PASSES, N_PASSES)
+            for i in range(4):
+                apply_relu(i)
+            for i in range(4):
+                turn_back(i)
+            for i in range(4):
+                divide(i)
+            for i in range(4):
+                store(N_BLOCKS - 1, i)

@@ -7,6 +7,7 @@ U32 = mybir.dt.uint32
 U8 = mybir.dt.uint8
 FP8X4 = mybir.dt.float8_e4m3fn_x4
 ADD = mybir.AluOpType.add
+MAX = mybir.AluOpType.max
 RELU = mybir.ActivationFunctionType.Relu
 AXIS_X = mybir.AxisListType.X
 
@@ -26,13 +27,15 @@ UNIT_PASSES = 2
 N_UNITS = N_PASSES // UNIT_PASSES
 K_UNIT = K_PASS * UNIT_PASSES
 PLANE = P * PACK
+LEAD = 2
+AHEAD = 4
 FLIP_BANKS = 5
 
 FLOPS = 2 * sum(N_ROWS // r for r in SCALES) * D * P
 
 
-def sums_on_tensor(b):
-    return b > 0
+def sums_on_tensor(b, h):
+    return b > 0 or h == N_UNITS - 1
 
 
 def tile_contractexpand_pa_k_kernel(tc, inputs_c_e, Ws, bs, out):
@@ -53,28 +56,31 @@ def tile_contractexpand_pa_k_kernel(tc, inputs_c_e, Ws, bs, out):
     ) as work, tc.psum_pool(name="flip", bufs=FLIP_BANKS) as flip_pool, tc.psum_pool(name="acc", bufs=1) as acc_pool:
         identity = keep.tile([P, P], F32, name="identity")
         make_identity(nc, identity[:])
-        adder_wide = keep.tile([P, QUADS], F32, name="adder_wide")
-        nc.vector.tensor_reduce(
-            out=adder_wide[:], in_=identity[:].rearrange("p (cc i) -> p cc i", i=QUAD), axis=AXIS_X, op=ADD
-        )
-        adder = keep.tile([P, QUADS], BF16, name="adder")
-        nc.vector.tensor_copy(out=adder[:], in_=adder_wide[:])
-
         w_codes = keep.tile([P, N_PASSES, len(SCALES), P], U32, name="w_codes", align_bytes=64)
         w_scales = keep.tile([P, N_PASSES, len(SCALES), P], U8, name="w_scales", align_bytes=64)
         codes12 = keep.tile([P, N_PASSES, P], U32, name="codes12", align_bytes=64)
         scales12 = keep.tile([P, N_PASSES, P], U8, name="scales12", align_bytes=64)
         run12 = keep.tile([P, N_PASSES, PLANE], F32, name="run12")
 
+        adder = keep.tile([P, QUADS], BF16, name="adder")
+        bias = keep.tile([P, len(SCALES)], F32, name="bias")
         bias_rows = keep.tile([P, P], BF16, name="bias_rows")
         nc.vector.memset(bias_rows[:], 0.0)
-        nc.sync.dma_start(out=bias_rows[0 : len(SCALES), :], in_=bs)
-        bias_wide = keep.tile([P, P], F32, name="bias_wide")
-        nc.vector.tensor_copy(out=bias_wide[:], in_=bias_rows[:])
-        bias_bank = flip_pool.tile([P, P], F32, name="bias_bank", tag="bank")
-        nc.tensor.transpose(bias_bank[:], bias_wide[:], identity[:])
-        bias = keep.tile([P, len(SCALES)], F32, name="bias")
-        nc.vector.tensor_copy(out=bias[:], in_=bias_bank[:, 0 : len(SCALES)])
+
+        def start_constants():
+            adder_wide = keep.tile([P, QUADS], F32, name="adder_wide")
+            nc.vector.tensor_reduce(
+                out=adder_wide[:], in_=identity[:].rearrange("p (cc i) -> p cc i", i=QUAD), axis=AXIS_X, op=ADD
+            )
+            nc.vector.tensor_copy(out=adder[:], in_=adder_wide[:])
+            nc.sync.dma_start(out=bias_rows[0 : len(SCALES), :], in_=bs)
+
+        def finish_constants():
+            bias_wide = keep.tile([P, P], F32, name="bias_wide")
+            nc.vector.tensor_copy(out=bias_wide[:], in_=bias_rows[:])
+            bias_bank = flip_pool.tile([P, P], F32, name="bias_bank", tag="bank")
+            nc.tensor.transpose(bias_bank[:], bias_wide[:], identity[:])
+            nc.scalar.copy(out=bias[:], in_=bias_bank[:, 0 : len(SCALES)])
 
         raws = {}
         banks = {}
@@ -83,7 +89,7 @@ def tile_contractexpand_pa_k_kernel(tc, inputs_c_e, Ws, bs, out):
         sums2 = {}
         sums4 = {}
         sums12 = {}
-        operands = {}
+        operands = {n: {} for n in range(len(units))}
         accs = {}
         relus = {}
         backs = {}
@@ -91,13 +97,16 @@ def tile_contractexpand_pa_k_kernel(tc, inputs_c_e, Ws, bs, out):
 
         def load(n):
             kind, b, h = units[n]
-            ks = slice(h * K_UNIT, (h + 1) * K_UNIT)
             raw = raw_pool.tile([P, TILES, K_UNIT], BF16, name="raw")
-            for i in range(QUAD):
-                if kind == "w":
-                    nc.sync.dma_start(out=raw[:, i, :], in_=Ws[i, :, ks])
-                else:
-                    nc.sync.dma_start(out=raw[i:P:QUAD, :, :], in_=x_rows[b, i, :, :, ks])
+            pieces = UNIT_PASSES if n < 2 else 1
+            for piece in range(pieces):
+                cols = slice(piece * K_UNIT // pieces, (piece + 1) * K_UNIT // pieces)
+                ks = slice(h * K_UNIT + cols.start, h * K_UNIT + cols.stop)
+                for i in range(QUAD):
+                    if kind == "w":
+                        nc.sync.dma_start(out=raw[:, i, cols], in_=Ws[i, :, ks])
+                    else:
+                        nc.sync.dma_start(out=raw[i:P:QUAD, :, cols], in_=x_rows[b, i, :, :, ks])
             raws[n] = raw
 
         def transpose(n):
@@ -116,13 +125,14 @@ def tile_contractexpand_pa_k_kernel(tc, inputs_c_e, Ws, bs, out):
 
         def copy_out(n):
             kind = units[n][0]
-            grouped = work.tile([P, UNIT_PASSES, QUAD, PLANE], BF16, name="grouped", align_bytes=64, bufs=3)
+            grouped = work.tile([P, UNIT_PASSES, QUAD, PLANE], BF16, name="grouped", align_bytes=64, bufs=4)
             words = grouped[:].bitcast(F32).rearrange("w q i (c u) -> w q i c u", u=2)
             for q in range(UNIT_PASSES):
                 for pair in range(TILES // 2):
                     bank = banks[n][q * (TILES // 2) + pair]
                     if kind == "w":
-                        nc.scalar.copy(
+                        copy = nc.vector.tensor_copy if n == 0 and pair == 1 else nc.scalar.copy
+                        copy(
                             out=words[:, q, 2 * pair : 2 * pair + 2, :, :],
                             in_=bank[:].rearrange("w u s o -> w s o u"),
                         )
@@ -135,7 +145,7 @@ def tile_contractexpand_pa_k_kernel(tc, inputs_c_e, Ws, bs, out):
             groupeds[n] = grouped
 
         def add_quads(n):
-            if not sums_on_tensor(units[n][1]):
+            if not sums_on_tensor(*units[n][1:]):
                 return
             raw = raws[n]
             quad_banks[n] = []
@@ -155,22 +165,23 @@ def tile_contractexpand_pa_k_kernel(tc, inputs_c_e, Ws, bs, out):
                 quad_banks[n].append(bank)
 
         def round_quads(n):
-            if not sums_on_tensor(units[n][1]):
+            if not sums_on_tensor(*units[n][1:]):
                 return
-            sum4_bf = work.tile([P, UNIT_PASSES, PLANE], BF16, name="sum4_bf", align_bytes=64)
+            sum4_bf = work.tile([P, UNIT_PASSES, PLANE], BF16, name="sum4_bf", align_bytes=64, bufs=4)
             sums4[n] = sum4_bf
             for q in range(UNIT_PASSES):
-                nc.scalar.copy(
-                    out=sum4_bf[:, q, :].rearrange("w (c v) -> w c v", v=PACK),
-                    in_=quad_banks[n][q][:].rearrange("w v c -> w c v"),
-                )
+                values = quad_banks[n][q][:].rearrange("w v c -> w c v")
+                nc.scalar.copy(out=sum4_bf[:, q, :].rearrange("w (c v) -> w c v", v=PACK), in_=values)
+                if units[n][1] == 0:
+                    carry = run12[:, units[n][2] * UNIT_PASSES + q, :]
+                    nc.scalar.copy(out=carry.rearrange("w (c v) -> w c v", v=PACK), in_=values)
 
         def carry_quads(n):
             b, h = units[n][1], units[n][2]
-            if not sums_on_tensor(b):
+            if b == 0 or not sums_on_tensor(b, h):
                 return
             if b == N_BLOCKS - 1:
-                sum12_bf = work.tile([P, UNIT_PASSES, PLANE], BF16, name="sum12_bf", align_bytes=64)
+                sum12_bf = work.tile([P, UNIT_PASSES, PLANE], BF16, name="sum12_bf", align_bytes=64, bufs=4)
                 sums12[n] = sum12_bf
             for q in range(UNIT_PASSES):
                 carry = run12[:, h * UNIT_PASSES + q, :].rearrange("w (c v) -> w c v", v=PACK)
@@ -181,10 +192,10 @@ def tile_contractexpand_pa_k_kernel(tc, inputs_c_e, Ws, bs, out):
                     out=target, in0=quad_banks[n][q][:].rearrange("w v c -> w c v"), in1=carry, op=ADD
                 )
 
-        def quantise(values, name):
+        def quantise(values, name, bufs):
             width = values.shape[1] // PACK
-            codes = work.tile([P, width], U32, name=name + "_codes", align_bytes=64, bufs=3)
-            scales = work.tile([P, width], U8, name=name + "_scales", align_bytes=64, bufs=3)
+            codes = work.tile([P, width], U32, name=name + "_codes", align_bytes=64, bufs=bufs)
+            scales = work.tile([P, width], U8, name=name + "_scales", align_bytes=64, bufs=bufs)
             nc.vector.quantize_mx(out=codes[:].bitcast(FP8X4), scales=scales[:], in_=values)
             return codes, scales
 
@@ -203,7 +214,7 @@ def tile_contractexpand_pa_k_kernel(tc, inputs_c_e, Ws, bs, out):
             rows = groupeds[n][:].rearrange("w q (m s) v -> w (q m) s v", s=2)
             sum2_bf = work.tile([P, UNIT_PASSES * 2, PLANE], BF16, name="sum2_bf", align_bytes=64)
             sums2[n] = sum2_bf
-            if sums_on_tensor(b):
+            if sums_on_tensor(b, h):
                 nc.vector.tensor_tensor(out=sum2_bf[:], in0=rows[:, :, 0, :], in1=rows[:, :, 1, :], op=ADD)
                 return
             sum2 = work.tile([P, UNIT_PASSES * 2, PLANE], F32, name="sum2")
@@ -212,16 +223,19 @@ def tile_contractexpand_pa_k_kernel(tc, inputs_c_e, Ws, bs, out):
             nc.vector.tensor_tensor(out=sum2_bf[:, 0:2, :], in0=rows[:, 0:2, 0, :], in1=rows[:, 0:2, 1, :], op=ADD)
             halves = sum2[:].rearrange("w (q m) v -> w q m v", m=2)
             nc.vector.tensor_tensor(out=run12[:, passes, :], in0=halves[:, :, 0, :], in1=halves[:, :, 1, :], op=ADD)
-            sum4_bf = work.tile([P, UNIT_PASSES, PLANE], BF16, name="sum4_bf", align_bytes=64)
+            sum4_bf = work.tile([P, UNIT_PASSES, PLANE], BF16, name="sum4_bf", align_bytes=64, bufs=4)
             nc.scalar.copy(out=sum4_bf[:], in_=run12[:, passes, :])
             sums4[n] = sum4_bf
 
         def quantise_rows(n):
-            operands[n] = {0: quantise(groupeds[n][:].rearrange("w q s v -> w (q s v)"), "x")}
+            operands[n][0] = quantise(groupeds[n][:].rearrange("w q s v -> w (q s v)"), "x", 3)
 
-        def quantise_sums(n):
+        def quantise_pairs(n):
+            operands[n][1] = quantise(sums2[n][:].rearrange("w a v -> w (a v)"), "sum2", 3)
+
+        def quantise_quads(n):
             b, h = units[n][1], units[n][2]
-            operands[n][2] = quantise(sums4[n][:].rearrange("w q v -> w (q v)"), "sum4")
+            operands[n][2] = quantise(sums4[n][:].rearrange("w q v -> w (q v)"), "sum4", 4)
             if b == N_BLOCKS - 1:
                 passes = slice(h * UNIT_PASSES, (h + 1) * UNIT_PASSES)
                 nc.vector.quantize_mx(
@@ -229,18 +243,16 @@ def tile_contractexpand_pa_k_kernel(tc, inputs_c_e, Ws, bs, out):
                     scales=scales12[:, passes, :].rearrange("w g c -> w (g c)"),
                     in_=sums12[n][:].rearrange("w q v -> w (q v)"),
                 )
-            operands[n][1] = quantise(sums2[n][:].rearrange("w a v -> w (a v)"), "sum2")
 
-        def multiply(n):
+        def multiply(n, i):
             h = units[n][2]
-            for i in range(len(operands[n])):
-                if h == 0:
-                    accs[i] = acc_pool.tile([P, QUAD // SCALES[i] * P], F32, name="acc%d" % i, tag="bank%d" % i)
-                codes, scales = operands[n][i]
-                width = codes.shape[1] // UNIT_PASSES
-                for q in range(UNIT_PASSES):
-                    cols = slice(q * width, (q + 1) * width)
-                    multiply_pass(i, h * UNIT_PASSES + q, codes[:, cols], scales[:, cols])
+            if h == 0:
+                accs[i] = acc_pool.tile([P, QUAD // SCALES[i] * P], F32, name="acc%d" % i, tag="bank%d" % i)
+            codes, scales = operands[n][i]
+            width = codes.shape[1] // UNIT_PASSES
+            for q in range(UNIT_PASSES):
+                cols = slice(q * width, (q + 1) * width)
+                multiply_pass(i, h * UNIT_PASSES + q, codes[:, cols], scales[:, cols])
 
         def multiply_pass(i, g, codes, scales):
             nc.tensor.matmul_mx(
@@ -253,22 +265,21 @@ def tile_contractexpand_pa_k_kernel(tc, inputs_c_e, Ws, bs, out):
                 stop=(g == N_PASSES - 1),
             )
 
-        def multiply12(first, last):
-            if first == 0:
-                accs[3] = flip_pool.tile([P, P], F32, name="acc12", tag="bank")
-            for g in range(first, last):
+        def multiply12():
+            accs[3] = flip_pool.tile([P, P], F32, name="acc12", tag="bank")
+            for g in range(N_PASSES):
                 multiply_pass(3, g, codes12[:, g, :], scales12[:, g, :])
 
-        def apply_relu(i):
+        def apply_relu(i, engine):
             planes = accs[i].shape[1] // P
-            relu = work.tile([P, planes, P], F32, name="relu%d" % i)
-            nc.scalar.activation(
-                out=relu[:].rearrange("o m c -> o (m c)"),
-                in_=accs[i][:],
-                func=RELU,
-                bias=bias[:, i : i + 1],
-                scale=1.0,
-            )
+            relu = work.tile([P, planes, P], F32, name="relu%d" % i, bufs=1)
+            flat = relu[:].rearrange("o m c -> o (m c)")
+            if engine == "vector":
+                nc.vector.tensor_scalar(
+                    out=flat, in0=accs[i][:], scalar1=bias[:, i : i + 1], scalar2=0.0, op0=ADD, op1=MAX
+                )
+            else:
+                nc.scalar.activation(out=flat, in_=accs[i][:], func=RELU, bias=bias[:, i : i + 1], scale=1.0)
             relus[i] = relu
 
         def turn_back(i):
@@ -278,15 +289,21 @@ def tile_contractexpand_pa_k_kernel(tc, inputs_c_e, Ws, bs, out):
                 nc.tensor.transpose(back[:, m, :], relus[i][:, m, :], identity[:])
             backs[i] = back
 
-        def divide(i):
+        def divide(i, engine):
             planes = relus[i].shape[1]
-            result = work.tile([P, planes, P], F32, name="result%d" % i)
-            nc.scalar.mul(out=result[:], in_=backs[i][:], mul=1.0 / SCALES[i])
+            result = work.tile([P, planes, P], F32, name="result%d" % i, bufs=1)
+            if engine == "vector":
+                nc.vector.tensor_scalar_mul(result[:], backs[i][:], 1.0 / SCALES[i])
+            else:
+                nc.scalar.mul(out=result[:], in_=backs[i][:], mul=1.0 / SCALES[i])
             results[i] = result
 
         def store(b, i):
             r = SCALES[i]
             first_row = b * QUAD if r <= QUAD else 0
+            if r == 1:
+                nc.sync.dma_start(out=out_rows[:, i, first_row : first_row + QUAD, :], in_=results[i][:])
+                return
             for m in range(results[i].shape[1]):
                 rows = slice(first_row + m * r, first_row + (m + 1) * r)
                 nc.sync.dma_start(
@@ -294,51 +311,70 @@ def tile_contractexpand_pa_k_kernel(tc, inputs_c_e, Ws, bs, out):
                 )
 
         last = len(units) - 1
+
+        def is_x(n, tensor_sums=None):
+            if not 0 <= n <= last or units[n][0] != "x":
+                return False
+            return tensor_sums is None or sums_on_tensor(*units[n][1:]) == tensor_sums
+
         with tc.manual_schedule():
-            for n in range(4):
+            load(0)
+            start_constants()
+            for n in range(1, AHEAD):
                 load(n)
-            for n in range(-1, len(units) + 2):
-                if n >= 0 and n + 4 <= last:
-                    load(n + 4)
+            for n in range(-LEAD, last + 1):
+                if n + LEAD > 0 and n + LEAD + AHEAD - 1 <= last:
+                    load(n + LEAD + AHEAD - 1)
                 done = n - 3
-                finished = 0 <= done <= last and units[done][0] == "x" and units[done][2] == N_UNITS - 1
+                finished = is_x(done) and units[done][2] == N_UNITS - 1
                 if finished:
                     for i in range(3):
-                        apply_relu(i)
-                if n + 1 <= last:
-                    transpose(n + 1)
-                    copy_out(n + 1)
-                    if units[n + 1][0] == "x":
-                        add_quads(n + 1)
-                        round_quads(n + 1)
-                if 0 <= n <= last and units[n][0] == "x":
+                        apply_relu(i, "scalar")
+                if n + LEAD <= last:
+                    transpose(n + LEAD)
+                    copy_out(n + LEAD)
+                if n == 1 - LEAD:
+                    finish_constants()
+                if is_x(n + LEAD, True):
+                    add_quads(n + LEAD)
+                    round_quads(n + LEAD)
+                if is_x(n):
                     add_pairs(n)
                     quantise_rows(n)
-                if 0 <= n <= last and units[n][0] == "w":
+                elif n >= 0:
                     quantise_weights(n)
-                if 0 <= n - 1 <= last and units[n - 1][0] == "x" and not sums_on_tensor(units[n - 1][1]):
-                    quantise_sums(n - 1)
-                if 0 <= n <= last and units[n][0] == "x" and sums_on_tensor(units[n][1]):
-                    quantise_sums(n)
-                if n + 1 <= last and units[n + 1][0] == "x":
-                    carry_quads(n + 1)
+                if is_x(n - 1, False):
+                    quantise_quads(n - 1)
+                    quantise_pairs(n - 1)
+                if is_x(n + 1, True):
+                    quantise_quads(n + 1)
+                if is_x(n, True):
+                    quantise_pairs(n)
+                if is_x(n + LEAD, True):
+                    carry_quads(n + LEAD)
                 if n == last:
-                    multiply12(0, N_PASSES - UNIT_PASSES)
-                if 0 <= n - 2 <= last and units[n - 2][0] == "x":
-                    multiply(n - 2)
+                    multiply12()
+                    apply_relu(3, "scalar")
+                if is_x(n - 2):
+                    for i in range(3):
+                        multiply(n - 2, i)
                 if finished:
                     for i in range(3):
                         turn_back(i)
                     for i in range(3):
-                        divide(i)
+                        divide(i, "scalar")
                     for i in range(3):
                         store(units[done][1], i)
-            multiply12(N_PASSES - UNIT_PASSES, N_PASSES)
-            for i in range(4):
-                apply_relu(i)
-            for i in range(4):
+            for i in range(3):
+                multiply(last - 1, i)
+            turn_back(3)
+            divide(3, "scalar")
+            store(N_BLOCKS - 1, 3)
+            tail = ((2, "scalar"), (0, "scalar"), (1, "vector"))
+            for i, engine in tail:
+                multiply(last, i)
+                apply_relu(i, engine)
+            for i, engine in tail:
                 turn_back(i)
-            for i in range(4):
-                divide(i)
-            for i in range(4):
+                divide(i, engine)
                 store(N_BLOCKS - 1, i)

@@ -35,7 +35,7 @@ FLOPS = 2 * sum(N_ROWS // r for r in SCALES) * D * P
 
 
 def sums_on_tensor(b, h):
-    return b > 0 or h == N_UNITS - 1
+    return b > 0 or h == 0
 
 
 def tile_contractexpand_pa_k_kernel(tc, inputs_c_e, Ws, bs, out):
@@ -45,8 +45,8 @@ def tile_contractexpand_pa_k_kernel(tc, inputs_c_e, Ws, bs, out):
 
     units = []
     for h in range(N_UNITS):
-        units.append(("w", 0, h))
         units.append(("x", 0, h))
+        units.append(("w", 0, h))
     for b in range(1, N_BLOCKS):
         for h in range(N_UNITS):
             units.append(("x", b, h))
@@ -131,14 +131,14 @@ def tile_contractexpand_pa_k_kernel(tc, inputs_c_e, Ws, bs, out):
                 for pair in range(TILES // 2):
                     bank = banks[n][q * (TILES // 2) + pair]
                     if kind == "w":
-                        copy = nc.vector.tensor_copy if n == 0 and pair == 1 else nc.scalar.copy
-                        copy(
+                        nc.scalar.copy(
                             out=words[:, q, 2 * pair : 2 * pair + 2, :, :],
                             in_=bank[:].rearrange("w u s o -> w s o u"),
                         )
                     else:
                         half = P // 2
-                        nc.scalar.copy(
+                        copy = nc.vector.tensor_copy if n == 0 and pair == 1 else nc.scalar.copy
+                        copy(
                             out=words[:, q, :, pair * half : (pair + 1) * half, :],
                             in_=bank[:].rearrange("w u s (cc i) -> w i (s cc) u", i=QUAD),
                         )
@@ -174,7 +174,7 @@ def tile_contractexpand_pa_k_kernel(tc, inputs_c_e, Ws, bs, out):
                 nc.scalar.copy(out=sum4_bf[:, q, :].rearrange("w (c v) -> w c v", v=PACK), in_=values)
                 if units[n][1] == 0:
                     carry = run12[:, units[n][2] * UNIT_PASSES + q, :]
-                    nc.scalar.copy(out=carry.rearrange("w (c v) -> w c v", v=PACK), in_=values)
+                    nc.vector.tensor_copy(out=carry.rearrange("w (c v) -> w c v", v=PACK), in_=values)
 
         def carry_quads(n):
             b, h = units[n][1], units[n][2]
@@ -338,6 +338,8 @@ def tile_contractexpand_pa_k_kernel(tc, inputs_c_e, Ws, bs, out):
                 if is_x(n + LEAD, True):
                     add_quads(n + LEAD)
                     round_quads(n + LEAD)
+                if n == last - 1:
+                    quantise_quads(last)
                 if is_x(n):
                     add_pairs(n)
                     quantise_rows(n)
@@ -346,7 +348,7 @@ def tile_contractexpand_pa_k_kernel(tc, inputs_c_e, Ws, bs, out):
                 if is_x(n - 1, False):
                     quantise_quads(n - 1)
                     quantise_pairs(n - 1)
-                if is_x(n + 1, True):
+                if is_x(n + 1, True) and n + 1 < last:
                     quantise_quads(n + 1)
                 if is_x(n, True):
                     quantise_pairs(n)
@@ -365,11 +367,11 @@ def tile_contractexpand_pa_k_kernel(tc, inputs_c_e, Ws, bs, out):
                         divide(i, "scalar")
                     for i in range(3):
                         store(units[done][1], i)
-            for i in range(3):
-                multiply(last - 1, i)
             turn_back(3)
             divide(3, "scalar")
             store(N_BLOCKS - 1, 3)
+            for i in range(3):
+                multiply(last - 1, i)
             tail = ((2, "scalar"), (0, "scalar"), (1, "vector"))
             for i, engine in tail:
                 multiply(last, i)

@@ -29,6 +29,7 @@ K_UNIT = K_PASS * UNIT_PASSES
 PLANE = P * PACK
 LEAD = 2
 AHEAD = 4
+GPSIMD_COLUMNS = 80
 FLIP_BANKS = 5
 
 FLOPS = 2 * sum(N_ROWS // r for r in SCALES) * D * P
@@ -212,10 +213,17 @@ def tile_contractexpand_pa_k_kernel(tc, inputs_c_e, Ws, bs, out):
             b, h = units[n][1], units[n][2]
             passes = slice(h * UNIT_PASSES, (h + 1) * UNIT_PASSES)
             rows = groupeds[n][:].rearrange("w q (m s) v -> w (q m) s v", s=2)
-            sum2_bf = work.tile([P, UNIT_PASSES * 2, PLANE], BF16, name="sum2_bf", align_bytes=64)
+            sum2_bf = work.tile([P, UNIT_PASSES * 2, PLANE], BF16, name="sum2_bf", align_bytes=64, bufs=1)
             sums2[n] = sum2_bf
             if sums_on_tensor(b, h):
-                nc.vector.tensor_tensor(out=sum2_bf[:], in0=rows[:, :, 0, :], in1=rows[:, :, 1, :], op=ADD)
+                ends = PLANE - (GPSIMD_COLUMNS if b > 0 else 0)
+                if b > 0:
+                    nc.gpsimd.tensor_tensor(
+                        out=sum2_bf[:, :, ends:], in0=rows[:, :, 0, ends:], in1=rows[:, :, 1, ends:], op=ADD
+                    )
+                nc.vector.tensor_tensor(
+                    out=sum2_bf[:, :, 0:ends], in0=rows[:, :, 0, 0:ends], in1=rows[:, :, 1, 0:ends], op=ADD
+                )
                 return
             sum2 = work.tile([P, UNIT_PASSES * 2, PLANE], F32, name="sum2")
             nc.vector.tensor_tensor(out=sum2[:], in0=rows[:, :, 0, :], in1=rows[:, :, 1, :], op=ADD)

@@ -29,6 +29,9 @@ K_UNIT = K_PASS * UNIT_PASSES
 PLANE = P * PACK
 LEAD = 2
 AHEAD = 4
+GPSIMD_FIRST = 32
+SCALAR_FIRST = 160
+GPSIMD_FOURS = 128
 GPSIMD_COLUMNS = 80
 FLIP_BANKS = 5
 
@@ -36,12 +39,13 @@ FLOPS = 2 * sum(N_ROWS // r for r in SCALES) * D * P
 
 
 def sums_on_tensor(b, h):
-    return b > 0 or h == 0
+    return b > 0
 
 
 def tile_contractexpand_pa_k_kernel(tc, inputs_c_e, Ws, bs, out):
     nc = tc.nc
     x_rows = inputs_c_e.rearrange("(t cc b i) k -> b i cc t k", t=TILES, cc=QUADS, b=N_BLOCKS)
+    x_planes = inputs_c_e.rearrange("(c b i) k -> b i c k", b=N_BLOCKS, i=QUAD)
     out_rows = out.rearrange("(i c j) o -> c i j o", i=len(SCALES), j=GROUP)
 
     units = []
@@ -87,6 +91,7 @@ def tile_contractexpand_pa_k_kernel(tc, inputs_c_e, Ws, bs, out):
         banks = {}
         groupeds = {}
         quad_banks = {}
+        pair_sums = {}
         sums2 = {}
         sums4 = {}
         sums12 = {}
@@ -106,6 +111,8 @@ def tile_contractexpand_pa_k_kernel(tc, inputs_c_e, Ws, bs, out):
                 for i in range(QUAD):
                     if kind == "w":
                         nc.sync.dma_start(out=raw[:, i, cols], in_=Ws[i, :, ks])
+                    elif not sums_on_tensor(b, h):
+                        nc.sync.dma_start(out=raw[:, i, cols], in_=x_planes[b, i, :, ks])
                     else:
                         nc.sync.dma_start(out=raw[i:P:QUAD, :, cols], in_=x_rows[b, i, :, :, ks])
             raws[n] = raw
@@ -125,21 +132,20 @@ def tile_contractexpand_pa_k_kernel(tc, inputs_c_e, Ws, bs, out):
                     banks[n].append(bank)
 
         def copy_out(n):
-            kind = units[n][0]
+            by_planes = units[n][0] == "w" or not sums_on_tensor(*units[n][1:])
             grouped = work.tile([P, UNIT_PASSES, QUAD, PLANE], BF16, name="grouped", align_bytes=64, bufs=4)
             words = grouped[:].bitcast(F32).rearrange("w q i (c u) -> w q i c u", u=2)
+            half = P // 2
             for q in range(UNIT_PASSES):
                 for pair in range(TILES // 2):
                     bank = banks[n][q * (TILES // 2) + pair]
-                    if kind == "w":
+                    if by_planes:
                         nc.scalar.copy(
                             out=words[:, q, 2 * pair : 2 * pair + 2, :, :],
                             in_=bank[:].rearrange("w u s o -> w s o u"),
                         )
                     else:
-                        half = P // 2
-                        copy = nc.vector.tensor_copy if n == 0 and pair == 1 else nc.scalar.copy
-                        copy(
+                        nc.scalar.copy(
                             out=words[:, q, :, pair * half : (pair + 1) * half, :],
                             in_=bank[:].rearrange("w u s (cc i) -> w i (s cc) u", i=QUAD),
                         )
@@ -209,31 +215,56 @@ def tile_contractexpand_pa_k_kernel(tc, inputs_c_e, Ws, bs, out):
                 in_=groupeds[n][:].rearrange("w q s v -> w (q s v)"),
             )
 
+        def add_from_psum(n):
+            sum2 = work.tile([P, UNIT_PASSES * 2, PLANE], F32, name="sum2")
+            for q in range(UNIT_PASSES):
+                for m in range(QUAD // 2):
+                    a = q * (QUAD // 2) + m
+                    odd = banks[n][a][:].bitcast(BF16).rearrange("w u s (c e) -> w s c u e", e=2)
+                    nc.vector.tensor_tensor(
+                        out=sum2[:, a, :].rearrange("w (c u e) -> w c u e", u=2, e=2),
+                        in0=odd[:, 1, :, :, :],
+                        in1=groupeds[n][:, q, 2 * m, :].rearrange("w (c u e) -> w c u e", u=2, e=2),
+                        op=ADD,
+                    )
+            pair_sums[n] = sum2
+
+        def add_fours(n):
+            h = units[n][2]
+            halves = pair_sums[n][:].rearrange("w (q m) v -> w q m v", m=2)
+            passes = slice(h * UNIT_PASSES, (h + 1) * UNIT_PASSES)
+            for engine, cols in ((nc.gpsimd, slice(GPSIMD_FOURS, PLANE)), (nc.vector, slice(0, GPSIMD_FOURS))):
+                engine.tensor_tensor(
+                    out=run12[:, passes, cols], in0=halves[:, :, 0, cols], in1=halves[:, :, 1, cols], op=ADD
+                )
+
+        def round_fours(n):
+            h = units[n][2]
+            sum4_bf = work.tile([P, UNIT_PASSES, PLANE], BF16, name="sum4_bf", align_bytes=64, bufs=4)
+            nc.scalar.copy(out=sum4_bf[:], in_=run12[:, h * UNIT_PASSES : (h + 1) * UNIT_PASSES, :])
+            sums4[n] = sum4_bf
+
         def add_pairs(n):
             b, h = units[n][1], units[n][2]
-            passes = slice(h * UNIT_PASSES, (h + 1) * UNIT_PASSES)
             rows = groupeds[n][:].rearrange("w q (m s) v -> w (q m) s v", s=2)
             sum2_bf = work.tile([P, UNIT_PASSES * 2, PLANE], BF16, name="sum2_bf", align_bytes=64, bufs=1)
             sums2[n] = sum2_bf
-            if sums_on_tensor(b, h):
-                ends = PLANE - (GPSIMD_COLUMNS if b > 0 else 0)
-                if b > 0:
-                    nc.gpsimd.tensor_tensor(
-                        out=sum2_bf[:, :, ends:], in0=rows[:, :, 0, ends:], in1=rows[:, :, 1, ends:], op=ADD
-                    )
-                nc.vector.tensor_tensor(
-                    out=sum2_bf[:, :, 0:ends], in0=rows[:, :, 0, 0:ends], in1=rows[:, :, 1, 0:ends], op=ADD
+            tensor_sums = sums_on_tensor(b, h)
+            scalar_ends = PLANE - (GPSIMD_COLUMNS if tensor_sums else GPSIMD_FIRST)
+            vector_ends = scalar_ends - (0 if tensor_sums else SCALAR_FIRST)
+            nc.gpsimd.tensor_tensor(
+                out=sum2_bf[:, :, scalar_ends:],
+                in0=rows[:, :, 0, scalar_ends:],
+                in1=rows[:, :, 1, scalar_ends:],
+                op=ADD,
+            )
+            if not tensor_sums:
+                nc.scalar.copy(
+                    out=sum2_bf[:, :, vector_ends:scalar_ends], in_=pair_sums[n][:, :, vector_ends:scalar_ends]
                 )
-                return
-            sum2 = work.tile([P, UNIT_PASSES * 2, PLANE], F32, name="sum2")
-            nc.vector.tensor_tensor(out=sum2[:], in0=rows[:, :, 0, :], in1=rows[:, :, 1, :], op=ADD)
-            nc.scalar.copy(out=sum2_bf[:, 2:4, :], in_=sum2[:, 2:4, :])
-            nc.vector.tensor_tensor(out=sum2_bf[:, 0:2, :], in0=rows[:, 0:2, 0, :], in1=rows[:, 0:2, 1, :], op=ADD)
-            halves = sum2[:].rearrange("w (q m) v -> w q m v", m=2)
-            nc.vector.tensor_tensor(out=run12[:, passes, :], in0=halves[:, :, 0, :], in1=halves[:, :, 1, :], op=ADD)
-            sum4_bf = work.tile([P, UNIT_PASSES, PLANE], BF16, name="sum4_bf", align_bytes=64, bufs=4)
-            nc.scalar.copy(out=sum4_bf[:], in_=run12[:, passes, :])
-            sums4[n] = sum4_bf
+            nc.vector.tensor_tensor(
+                out=sum2_bf[:, :, 0:vector_ends], in0=rows[:, :, 0, 0:vector_ends], in1=rows[:, :, 1, 0:vector_ends], op=ADD
+            )
 
         def quantise_rows(n):
             operands[n][0] = quantise(groupeds[n][:].rearrange("w q s v -> w (q s v)"), "x", 3)
@@ -243,7 +274,7 @@ def tile_contractexpand_pa_k_kernel(tc, inputs_c_e, Ws, bs, out):
 
         def quantise_quads(n):
             b, h = units[n][1], units[n][2]
-            operands[n][2] = quantise(sums4[n][:].rearrange("w q v -> w (q v)"), "sum4", 4)
+            operands[n][2] = quantise(sums4[n][:].rearrange("w q v -> w (q v)"), "sum4", 6)
             if b == N_BLOCKS - 1:
                 passes = slice(h * UNIT_PASSES, (h + 1) * UNIT_PASSES)
                 nc.vector.quantize_mx(
@@ -335,26 +366,34 @@ def tile_contractexpand_pa_k_kernel(tc, inputs_c_e, Ws, bs, out):
                     load(n + LEAD + AHEAD - 1)
                 done = n - 3
                 finished = is_x(done) and units[done][2] == N_UNITS - 1
+                scales = range(2 if finished and is_x(done, False) else 3)
                 if finished:
-                    for i in range(3):
+                    for i in scales:
                         apply_relu(i, "scalar")
                 if n + LEAD <= last:
                     transpose(n + LEAD)
                     copy_out(n + LEAD)
+                if is_x(n - 1, False):
+                    round_fours(n - 1)
                 if n == 1 - LEAD:
                     finish_constants()
                 if is_x(n + LEAD, True):
                     add_quads(n + LEAD)
                     round_quads(n + LEAD)
+                if is_x(n + LEAD, False):
+                    add_from_psum(n + LEAD)
                 if n == last - 1:
                     quantise_quads(last)
                 if is_x(n):
                     add_pairs(n)
+                    if is_x(n, False):
+                        add_fours(n)
                     quantise_rows(n)
                 elif n >= 0:
                     quantise_weights(n)
+                if is_x(n - 3, False):
+                    quantise_quads(n - 3)
                 if is_x(n - 1, False):
-                    quantise_quads(n - 1)
                     quantise_pairs(n - 1)
                 if is_x(n + 1, True) and n + 1 < last:
                     quantise_quads(n + 1)
@@ -365,16 +404,26 @@ def tile_contractexpand_pa_k_kernel(tc, inputs_c_e, Ws, bs, out):
                 if n == last:
                     multiply12()
                     apply_relu(3, "scalar")
+                late = is_x(n - 4, False)
+                if late:
+                    multiply(n - 4, 2)
+                late = late and units[n - 4][2] == N_UNITS - 1
+                if late:
+                    apply_relu(2, "scalar")
                 if is_x(n - 2):
-                    for i in range(3):
+                    for i in range(3 if is_x(n - 2, True) else 2):
                         multiply(n - 2, i)
                 if finished:
-                    for i in range(3):
+                    for i in scales:
                         turn_back(i)
-                    for i in range(3):
+                    for i in scales:
                         divide(i, "scalar")
-                    for i in range(3):
+                    for i in scales:
                         store(units[done][1], i)
+                if late:
+                    turn_back(2)
+                    divide(2, "scalar")
+                    store(0, 2)
             turn_back(3)
             divide(3, "scalar")
             store(N_BLOCKS - 1, 3)

@@ -28,12 +28,12 @@ N_UNITS = N_PASSES // UNIT_PASSES
 K_UNIT = K_PASS * UNIT_PASSES
 PLANE = P * PACK
 LEAD = 2
-AHEAD = 4
-GPSIMD_FIRST = 32
-SCALAR_FIRST = 160
-GPSIMD_FOURS = 128
-GPSIMD_COLUMNS = 80
-FLIP_BANKS = 5
+AHEAD = 3
+GPSIMD_FIRST = 16
+SCALAR_FIRST = 176
+GPSIMD_FOURS = 160
+GPSIMD_COLUMNS = 64
+FLIP_BANKS = 6
 
 FLOPS = 2 * sum(N_ROWS // r for r in SCALES) * D * P
 
@@ -56,7 +56,7 @@ def tile_contractexpand_pa_k_kernel(tc, inputs_c_e, Ws, bs, out):
         for h in range(N_UNITS):
             units.append(("x", b, h))
 
-    with tc.tile_pool(name="keep", bufs=1) as keep, tc.tile_pool(name="raw", bufs=5) as raw_pool, tc.tile_pool(
+    with tc.tile_pool(name="keep", bufs=1) as keep, tc.tile_pool(name="raw", bufs=4) as raw_pool, tc.tile_pool(
         name="work", bufs=2
     ) as work, tc.psum_pool(name="flip", bufs=FLIP_BANKS) as flip_pool, tc.psum_pool(name="acc", bufs=1) as acc_pool:
         identity = keep.tile([P, P], F32, name="identity")
@@ -65,6 +65,8 @@ def tile_contractexpand_pa_k_kernel(tc, inputs_c_e, Ws, bs, out):
         w_scales = keep.tile([P, N_PASSES, len(SCALES), P], U8, name="w_scales", align_bytes=64)
         codes12 = keep.tile([P, N_PASSES, P], U32, name="codes12", align_bytes=64)
         scales12 = keep.tile([P, N_PASSES, P], U8, name="scales12", align_bytes=64)
+        codes4 = keep.tile([P, 2, N_PASSES, P], U32, name="codes4", align_bytes=64)
+        scales4 = keep.tile([P, 2, N_PASSES, P], U8, name="scales4", align_bytes=64)
         run12 = keep.tile([P, N_PASSES, PLANE], F32, name="run12")
 
         adder = keep.tile([P, QUADS], BF16, name="adder")
@@ -251,13 +253,16 @@ def tile_contractexpand_pa_k_kernel(tc, inputs_c_e, Ws, bs, out):
             sums2[n] = sum2_bf
             tensor_sums = sums_on_tensor(b, h)
             scalar_ends = PLANE - (GPSIMD_COLUMNS if tensor_sums else GPSIMD_FIRST)
+            if n == len(units) - 1:
+                scalar_ends = PLANE
             vector_ends = scalar_ends - (0 if tensor_sums else SCALAR_FIRST)
-            nc.gpsimd.tensor_tensor(
-                out=sum2_bf[:, :, scalar_ends:],
-                in0=rows[:, :, 0, scalar_ends:],
-                in1=rows[:, :, 1, scalar_ends:],
-                op=ADD,
-            )
+            if scalar_ends < PLANE:
+                nc.gpsimd.tensor_tensor(
+                    out=sum2_bf[:, :, scalar_ends:],
+                    in0=rows[:, :, 0, scalar_ends:],
+                    in1=rows[:, :, 1, scalar_ends:],
+                    op=ADD,
+                )
             if not tensor_sums:
                 nc.scalar.copy(
                     out=sum2_bf[:, :, vector_ends:scalar_ends], in_=pair_sums[n][:, :, vector_ends:scalar_ends]
@@ -274,9 +279,13 @@ def tile_contractexpand_pa_k_kernel(tc, inputs_c_e, Ws, bs, out):
 
         def quantise_quads(n):
             b, h = units[n][1], units[n][2]
-            operands[n][2] = quantise(sums4[n][:].rearrange("w q v -> w (q v)"), "sum4", 6)
+            passes = slice(h * UNIT_PASSES, (h + 1) * UNIT_PASSES)
+            nc.vector.quantize_mx(
+                out=codes4[:, b % 2, passes, :].rearrange("w g c -> w (g c)").bitcast(FP8X4),
+                scales=scales4[:, b % 2, passes, :].rearrange("w g c -> w (g c)"),
+                in_=sums4[n][:].rearrange("w q v -> w (q v)"),
+            )
             if b == N_BLOCKS - 1:
-                passes = slice(h * UNIT_PASSES, (h + 1) * UNIT_PASSES)
                 nc.vector.quantize_mx(
                     out=codes12[:, passes, :].rearrange("w g c -> w (g c)").bitcast(FP8X4),
                     scales=scales12[:, passes, :].rearrange("w g c -> w (g c)"),
@@ -309,16 +318,21 @@ def tile_contractexpand_pa_k_kernel(tc, inputs_c_e, Ws, bs, out):
             for g in range(N_PASSES):
                 multiply_pass(3, g, codes12[:, g, :], scales12[:, g, :])
 
-        def apply_relu(i, engine):
-            planes = accs[i].shape[1] // P
-            relu = work.tile([P, planes, P], F32, name="relu%d" % i, bufs=1)
+        def multiply4(b):
+            accs[2] = flip_pool.tile([P, P], F32, name="acc4", tag="bank")
+            for g in range(N_PASSES):
+                multiply_pass(2, g, codes4[:, b % 2, g, :], scales4[:, b % 2, g, :])
+
+        def apply_relu(i, engine, part=None):
+            part = part or slice(0, accs[i].shape[1] // P)
+            planes = part.stop - part.start
+            relu = work.tile([P, planes, P], F32, name="relu%d_%d" % (i, part.start), bufs=1)
             flat = relu[:].rearrange("o m c -> o (m c)")
+            values = accs[i][:, part.start * P : part.stop * P]
             if engine == "vector":
-                nc.vector.tensor_scalar(
-                    out=flat, in0=accs[i][:], scalar1=bias[:, i : i + 1], scalar2=0.0, op0=ADD, op1=MAX
-                )
+                nc.vector.tensor_scalar(out=flat, in0=values, scalar1=bias[:, i : i + 1], scalar2=0.0, op0=ADD, op1=MAX)
             else:
-                nc.scalar.activation(out=flat, in_=accs[i][:], func=RELU, bias=bias[:, i : i + 1], scale=1.0)
+                nc.scalar.activation(out=flat, in_=values, func=RELU, bias=bias[:, i : i + 1], scale=1.0)
             relus[i] = relu
 
         def turn_back(i):
@@ -330,18 +344,19 @@ def tile_contractexpand_pa_k_kernel(tc, inputs_c_e, Ws, bs, out):
 
         def divide(i, engine):
             planes = relus[i].shape[1]
-            result = work.tile([P, planes, P], F32, name="result%d" % i, bufs=1)
+            result = work.tile([P, planes, P], F32, name="result%d" % i, bufs=2 if i == 0 else 1)
             if engine == "vector":
                 nc.vector.tensor_scalar_mul(result[:], backs[i][:], 1.0 / SCALES[i])
             else:
                 nc.scalar.mul(out=result[:], in_=backs[i][:], mul=1.0 / SCALES[i])
             results[i] = result
 
-        def store(b, i):
+        def store(b, i, first_plane=0):
             r = SCALES[i]
-            first_row = b * QUAD if r <= QUAD else 0
+            first_row = (b * QUAD if r <= QUAD else 0) + first_plane
             if r == 1:
-                nc.sync.dma_start(out=out_rows[:, i, first_row : first_row + QUAD, :], in_=results[i][:])
+                rows = slice(first_row, first_row + results[i].shape[1])
+                nc.sync.dma_start(out=out_rows[:, i, rows, :], in_=results[i][:])
                 return
             for m in range(results[i].shape[1]):
                 rows = slice(first_row + m * r, first_row + (m + 1) * r)
@@ -356,6 +371,11 @@ def tile_contractexpand_pa_k_kernel(tc, inputs_c_e, Ws, bs, out):
                 return False
             return tensor_sums is None or sums_on_tensor(*units[n][1:]) == tensor_sums
 
+        fours = {}
+        for n in range(len(units)):
+            if is_x(n) and units[n][2] == N_UNITS - 1:
+                fours[n if sums_on_tensor(*units[n][1:]) else n + 4] = units[n][1]
+
         with tc.manual_schedule():
             load(0)
             start_constants()
@@ -366,10 +386,11 @@ def tile_contractexpand_pa_k_kernel(tc, inputs_c_e, Ws, bs, out):
                     load(n + LEAD + AHEAD - 1)
                 done = n - 3
                 finished = is_x(done) and units[done][2] == N_UNITS - 1
-                scales = range(2 if finished and is_x(done, False) else 3)
                 if finished:
-                    for i in scales:
+                    for i in range(2):
                         apply_relu(i, "scalar")
+                if n - 1 in fours:
+                    apply_relu(2, "scalar")
                 if n + LEAD <= last:
                     transpose(n + LEAD)
                     copy_out(n + LEAD)
@@ -404,36 +425,41 @@ def tile_contractexpand_pa_k_kernel(tc, inputs_c_e, Ws, bs, out):
                 if n == last:
                     multiply12()
                     apply_relu(3, "scalar")
-                late = is_x(n - 4, False)
-                if late:
-                    multiply(n - 4, 2)
-                late = late and units[n - 4][2] == N_UNITS - 1
-                if late:
-                    apply_relu(2, "scalar")
+                if n in fours:
+                    multiply4(fours[n])
                 if is_x(n - 2):
-                    for i in range(3 if is_x(n - 2, True) else 2):
+                    for i in range(2):
                         multiply(n - 2, i)
                 if finished:
-                    for i in scales:
+                    for i in range(2):
                         turn_back(i)
-                    for i in scales:
+                    for i in range(2):
                         divide(i, "scalar")
-                    for i in scales:
+                    for i in range(2):
                         store(units[done][1], i)
-                if late:
+                if n - 1 in fours:
                     turn_back(2)
                     divide(2, "scalar")
-                    store(0, 2)
-            turn_back(3)
-            divide(3, "scalar")
-            store(N_BLOCKS - 1, 3)
-            for i in range(3):
-                multiply(last - 1, i)
-            tail = ((2, "scalar"), (0, "scalar"), (1, "vector"))
-            for i, engine in tail:
-                multiply(last, i)
-                apply_relu(i, engine)
-            for i, engine in tail:
+                    store(fours[n - 1], 2)
+            apply_relu(2, "scalar")
+            for i in (3, 2):
                 turn_back(i)
-                divide(i, engine)
+                divide(i, "scalar")
                 store(N_BLOCKS - 1, i)
+            for n in (last - 1, last):
+                for i in range(2):
+                    multiply(n, i)
+            halves = (slice(0, QUAD // 2), slice(QUAD // 2, QUAD))
+            parts = []
+            for part in halves:
+                apply_relu(0, "scalar", part)
+                parts.append(relus[0])
+            apply_relu(1, "vector")
+            for part, relu in zip(halves, parts):
+                relus[0] = relu
+                turn_back(0)
+                divide(0, "scalar")
+                store(N_BLOCKS - 1, 0, part.start)
+            turn_back(1)
+            divide(1, "vector")
+            store(N_BLOCKS - 1, 1)

import concourse.mybir as mybir
from concourse.masks import make_identity

F32 = mybir.dt.float32
BF16 = mybir.dt.bfloat16
U32 = mybir.dt.uint32
U8 = mybir.dt.uint8
FP8X4 = mybir.dt.float8_e4m3fn_x4
ADD = mybir.AluOpType.add
MAX = mybir.AluOpType.max
RELU = mybir.ActivationFunctionType.Relu
AXIS_X = mybir.AxisListType.X

P = 128
N_ROWS = 1536
D = 8192
SCALES = (1, 2, 4, 12)
GROUP = 12
QUAD = 4
N_BLOCKS = GROUP // QUAD
TILES = 4
QUADS = P // QUAD
PACK = 4
K_PASS = P * PACK
N_PASSES = D // K_PASS
UNIT_PASSES = 2
N_UNITS = N_PASSES // UNIT_PASSES
K_UNIT = K_PASS * UNIT_PASSES
PLANE = P * PACK
LEAD = 2
AHEAD = 3
GPSIMD_FIRST = 16
SCALAR_FIRST = 176
GPSIMD_FOURS = 160
GPSIMD_COLUMNS = 64
FLIP_BANKS = 6

FLOPS = 2 * sum(N_ROWS // r for r in SCALES) * D * P


def sums_on_tensor(b, h):
    return b > 0


def tile_contractexpand_pa_k_kernel(tc, inputs_c_e, Ws, bs, out):
    nc = tc.nc
    x_rows = inputs_c_e.rearrange("(t cc b i) k -> b i cc t k", t=TILES, cc=QUADS, b=N_BLOCKS)
    x_planes = inputs_c_e.rearrange("(c b i) k -> b i c k", b=N_BLOCKS, i=QUAD)
    out_rows = out.rearrange("(i c j) o -> c i j o", i=len(SCALES), j=GROUP)

    units = []
    for h in range(N_UNITS):
        units.append(("x", 0, h))
        units.append(("w", 0, h))
    for b in range(1, N_BLOCKS):
        for h in range(N_UNITS):
            units.append(("x", b, h))

    with tc.tile_pool(name="keep", bufs=1) as keep, tc.tile_pool(name="raw", bufs=4) as raw_pool, tc.tile_pool(
        name="work", bufs=2
    ) as work, tc.psum_pool(name="flip", bufs=FLIP_BANKS) as flip_pool, tc.psum_pool(name="acc", bufs=1) as acc_pool:
        identity = keep.tile([P, P], F32, name="identity")
        make_identity(nc, identity[:])
        w_codes = keep.tile([P, N_PASSES, len(SCALES), P], U32, name="w_codes", align_bytes=64)
        w_scales = keep.tile([P, N_PASSES, len(SCALES), P], U8, name="w_scales", align_bytes=64)
        codes12 = keep.tile([P, N_PASSES, P], U32, name="codes12", align_bytes=64)
        scales12 = keep.tile([P, N_PASSES, P], U8, name="scales12", align_bytes=64)
        codes4 = keep.tile([P, 2, N_PASSES, P], U32, name="codes4", align_bytes=64)
        scales4 = keep.tile([P, 2, N_PASSES, P], U8, name="scales4", align_bytes=64)
        run12 = keep.tile([P, N_PASSES, PLANE], F32, name="run12")

        adder = keep.tile([P, QUADS], BF16, name="adder")
        bias = keep.tile([P, len(SCALES)], F32, name="bias")
        bias_rows = keep.tile([P, P], BF16, name="bias_rows")
        nc.vector.memset(bias_rows[:], 0.0)

        def start_constants():
            adder_wide = keep.tile([P, QUADS], F32, name="adder_wide")
            nc.vector.tensor_reduce(
                out=adder_wide[:], in_=identity[:].rearrange("p (cc i) -> p cc i", i=QUAD), axis=AXIS_X, op=ADD
            )
            nc.vector.tensor_copy(out=adder[:], in_=adder_wide[:])
            nc.sync.dma_start(out=bias_rows[0 : len(SCALES), :], in_=bs)

        def finish_constants():
            bias_wide = keep.tile([P, P], F32, name="bias_wide")
            nc.vector.tensor_copy(out=bias_wide[:], in_=bias_rows[:])
            bias_bank = flip_pool.tile([P, P], F32, name="bias_bank", tag="bank")
            nc.tensor.transpose(bias_bank[:], bias_wide[:], identity[:])
            nc.scalar.copy(out=bias[:], in_=bias_bank[:, 0 : len(SCALES)])

        raws = {}
        banks = {}
        groupeds = {}
        quad_banks = {}
        pair_sums = {}
        sums2 = {}
        sums4 = {}
        sums12 = {}
        operands = {n: {} for n in range(len(units))}
        accs = {}
        relus = {}
        backs = {}
        results = {}

        def load(n):
            kind, b, h = units[n]
            raw = raw_pool.tile([P, TILES, K_UNIT], BF16, name="raw")
            pieces = UNIT_PASSES if n < 2 else 1
            for piece in range(pieces):
                cols = slice(piece * K_UNIT // pieces, (piece + 1) * K_UNIT // pieces)
                ks = slice(h * K_UNIT + cols.start, h * K_UNIT + cols.stop)
                for i in range(QUAD):
                    if kind == "w":
                        nc.sync.dma_start(out=raw[:, i, cols], in_=Ws[i, :, ks])
                    elif not sums_on_tensor(b, h):
                        nc.sync.dma_start(out=raw[:, i, cols], in_=x_planes[b, i, :, ks])
                    else:
                        nc.sync.dma_start(out=raw[i:P:QUAD, :, cols], in_=x_rows[b, i, :, :, ks])
            raws[n] = raw

        def transpose(n):
            words = raws[n][:].bitcast(F32)
            banks[n] = []
            for q in range(UNIT_PASSES):
                for pair in range(TILES // 2):
                    bank = flip_pool.tile([P, 2, 2, P], F32, name="bank")
                    for s in range(2):
                        for u in range(2):
                            first = (2 * q + u) * P
                            nc.tensor.transpose(
                                bank[:, u, s, :], words[:, 2 * pair + s, first : first + P], identity[:]
                            )
                    banks[n].append(bank)

        def copy_out(n):
            by_planes = units[n][0] == "w" or not sums_on_tensor(*units[n][1:])
            grouped = work.tile([P, UNIT_PASSES, QUAD, PLANE], BF16, name="grouped", align_bytes=64, bufs=4)
            words = grouped[:].bitcast(F32).rearrange("w q i (c u) -> w q i c u", u=2)
            half = P // 2
            for q in range(UNIT_PASSES):
                for pair in range(TILES // 2):
                    bank = banks[n][q * (TILES // 2) + pair]
                    if by_planes:
                        nc.scalar.copy(
                            out=words[:, q, 2 * pair : 2 * pair + 2, :, :],
                            in_=bank[:].rearrange("w u s o -> w s o u"),
                        )
                    else:
                        nc.scalar.copy(
                            out=words[:, q, :, pair * half : (pair + 1) * half, :],
                            in_=bank[:].rearrange("w u s (cc i) -> w i (s cc) u", i=QUAD),
                        )
            groupeds[n] = grouped

        def add_quads(n):
            if not sums_on_tensor(*units[n][1:]):
                return
            raw = raws[n]
            quad_banks[n] = []
            for q in range(UNIT_PASSES):
                bank = flip_pool.tile([P, PACK, P], F32, name="quad_bank", tag="bank")
                for t in range(TILES):
                    for u in range(2):
                        for e in range(2):
                            first = q * K_PASS + u * 2 * P + e
                            nc.tensor.matmul(
                                bank[:, 2 * u + e, t * QUADS : (t + 1) * QUADS],
                                lhsT=raw[:, t, first : (2 * q + u + 1) * 2 * P : 2],
                                rhs=adder[:],
                                start=True,
                                stop=True,
                            )
                quad_banks[n].append(bank)

        def round_quads(n):
            if not sums_on_tensor(*units[n][1:]):
                return
            sum4_bf = work.tile([P, UNIT_PASSES, PLANE], BF16, name="sum4_bf", align_bytes=64, bufs=4)
            sums4[n] = sum4_bf
            for q in range(UNIT_PASSES):
                values = quad_banks[n][q][:].rearrange("w v c -> w c v")
                nc.scalar.copy(out=sum4_bf[:, q, :].rearrange("w (c v) -> w c v", v=PACK), in_=values)
                if units[n][1] == 0:
                    carry = run12[:, units[n][2] * UNIT_PASSES + q, :]
                    nc.vector.tensor_copy(out=carry.rearrange("w (c v) -> w c v", v=PACK), in_=values)

        def carry_quads(n):
            b, h = units[n][1], units[n][2]
            if b == 0 or not sums_on_tensor(b, h):
                return
            if b == N_BLOCKS - 1:
                sum12_bf = work.tile([P, UNIT_PASSES, PLANE], BF16, name="sum12_bf", align_bytes=64, bufs=4)
                sums12[n] = sum12_bf
            for q in range(UNIT_PASSES):
                carry = run12[:, h * UNIT_PASSES + q, :].rearrange("w (c v) -> w c v", v=PACK)
                target = carry
                if b == N_BLOCKS - 1:
                    target = sum12_bf[:, q, :].rearrange("w (c v) -> w c v", v=PACK)
                nc.vector.tensor_tensor(
                    out=target, in0=quad_banks[n][q][:].rearrange("w v c -> w c v"), in1=carry, op=ADD
                )

        def quantise(values, name, bufs):
            width = values.shape[1] // PACK
            codes = work.tile([P, width], U32, name=name + "_codes", align_bytes=64, bufs=bufs)
            scales = work.tile([P, width], U8, name=name + "_scales", align_bytes=64, bufs=bufs)
            nc.vector.quantize_mx(out=codes[:].bitcast(FP8X4), scales=scales[:], in_=values)
            return codes, scales

        def quantise_weights(n):
            h = units[n][2]
            passes = slice(h * UNIT_PASSES, (h + 1) * UNIT_PASSES)
            nc.vector.quantize_mx(
                out=w_codes[:, passes, :, :].rearrange("w g i o -> w (g i o)").bitcast(FP8X4),
                scales=w_scales[:, passes, :, :].rearrange("w g i o -> w (g i o)"),
                in_=groupeds[n][:].rearrange("w q s v -> w (q s v)"),
            )

        def add_from_psum(n):
            sum2 = work.tile([P, UNIT_PASSES * 2, PLANE], F32, name="sum2")
            for q in range(UNIT_PASSES):
                for m in range(QUAD // 2):
                    a = q * (QUAD // 2) + m
                    odd = banks[n][a][:].bitcast(BF16).rearrange("w u s (c e) -> w s c u e", e=2)
                    nc.vector.tensor_tensor(
                        out=sum2[:, a, :].rearrange("w (c u e) -> w c u e", u=2, e=2),
                        in0=odd[:, 1, :, :, :],
                        in1=groupeds[n][:, q, 2 * m, :].rearrange("w (c u e) -> w c u e", u=2, e=2),
                        op=ADD,
                    )
            pair_sums[n] = sum2

        def add_fours(n):
            h = units[n][2]
            halves = pair_sums[n][:].rearrange("w (q m) v -> w q m v", m=2)
            passes = slice(h * UNIT_PASSES, (h + 1) * UNIT_PASSES)
            for engine, cols in ((nc.gpsimd, slice(GPSIMD_FOURS, PLANE)), (nc.vector, slice(0, GPSIMD_FOURS))):
                engine.tensor_tensor(
                    out=run12[:, passes, cols], in0=halves[:, :, 0, cols], in1=halves[:, :, 1, cols], op=ADD
                )

        def round_fours(n):
            h = units[n][2]
            sum4_bf = work.tile([P, UNIT_PASSES, PLANE], BF16, name="sum4_bf", align_bytes=64, bufs=4)
            nc.scalar.copy(out=sum4_bf[:], in_=run12[:, h * UNIT_PASSES : (h + 1) * UNIT_PASSES, :])
            sums4[n] = sum4_bf

        def add_pairs(n):
            b, h = units[n][1], units[n][2]
            rows = groupeds[n][:].rearrange("w q (m s) v -> w (q m) s v", s=2)
            sum2_bf = work.tile([P, UNIT_PASSES * 2, PLANE], BF16, name="sum2_bf", align_bytes=64, bufs=1)
            sums2[n] = sum2_bf
            tensor_sums = sums_on_tensor(b, h)
            scalar_ends = PLANE - (GPSIMD_COLUMNS if tensor_sums else GPSIMD_FIRST)
            if n == len(units) - 1:
                scalar_ends = PLANE
            vector_ends = scalar_ends - (0 if tensor_sums else SCALAR_FIRST)
            if scalar_ends < PLANE:
                nc.gpsimd.tensor_tensor(
                    out=sum2_bf[:, :, scalar_ends:],
                    in0=rows[:, :, 0, scalar_ends:],
                    in1=rows[:, :, 1, scalar_ends:],
                    op=ADD,
                )
            if not tensor_sums:
                nc.scalar.copy(
                    out=sum2_bf[:, :, vector_ends:scalar_ends], in_=pair_sums[n][:, :, vector_ends:scalar_ends]
                )
            nc.vector.tensor_tensor(
                out=sum2_bf[:, :, 0:vector_ends], in0=rows[:, :, 0, 0:vector_ends], in1=rows[:, :, 1, 0:vector_ends], op=ADD
            )

        def quantise_rows(n):
            operands[n][0] = quantise(groupeds[n][:].rearrange("w q s v -> w (q s v)"), "x", 3)

        def quantise_pairs(n):
            operands[n][1] = quantise(sums2[n][:].rearrange("w a v -> w (a v)"), "sum2", 3)

        def quantise_quads(n):
            b, h = units[n][1], units[n][2]
            passes = slice(h * UNIT_PASSES, (h + 1) * UNIT_PASSES)
            nc.vector.quantize_mx(
                out=codes4[:, b % 2, passes, :].rearrange("w g c -> w (g c)").bitcast(FP8X4),
                scales=scales4[:, b % 2, passes, :].rearrange("w g c -> w (g c)"),
                in_=sums4[n][:].rearrange("w q v -> w (q v)"),
            )
            if b == N_BLOCKS - 1:
                nc.vector.quantize_mx(
                    out=codes12[:, passes, :].rearrange("w g c -> w (g c)").bitcast(FP8X4),
                    scales=scales12[:, passes, :].rearrange("w g c -> w (g c)"),
                    in_=sums12[n][:].rearrange("w q v -> w (q v)"),
                )

        def multiply(n, i):
            h = units[n][2]
            if h == 0:
                accs[i] = acc_pool.tile([P, QUAD // SCALES[i] * P], F32, name="acc%d" % i, tag="bank%d" % i)
            codes, scales = operands[n][i]
            width = codes.shape[1] // UNIT_PASSES
            for q in range(UNIT_PASSES):
                cols = slice(q * width, (q + 1) * width)
                multiply_pass(i, h * UNIT_PASSES + q, codes[:, cols], scales[:, cols])

        def multiply_pass(i, g, codes, scales):
            nc.tensor.matmul_mx(
                out=accs[i][:],
                lhsT=w_codes[:, g, i, :].bitcast(FP8X4),
                lhsT_scale=w_scales[:, g, i, :],
                rhs=codes.bitcast(FP8X4),
                rhs_scale=scales,
                start=(g == 0),
                stop=(g == N_PASSES - 1),
            )

        def multiply12():
            accs[3] = flip_pool.tile([P, P], F32, name="acc12", tag="bank")
            for g in range(N_PASSES):
                multiply_pass(3, g, codes12[:, g, :], scales12[:, g, :])

        def multiply4(b):
            accs[2] = flip_pool.tile([P, P], F32, name="acc4", tag="bank")
            for g in range(N_PASSES):
                multiply_pass(2, g, codes4[:, b % 2, g, :], scales4[:, b % 2, g, :])

        def apply_relu(i, engine, part=None):
            part = part or slice(0, accs[i].shape[1] // P)
            planes = part.stop - part.start
            relu = work.tile([P, planes, P], F32, name="relu%d_%d" % (i, part.start), bufs=1)
            flat = relu[:].rearrange("o m c -> o (m c)")
            values = accs[i][:, part.start * P : part.stop * P]
            if engine == "vector":
                nc.vector.tensor_scalar(out=flat, in0=values, scalar1=bias[:, i : i + 1], scalar2=0.0, op0=ADD, op1=MAX)
            else:
                nc.scalar.activation(out=flat, in_=values, func=RELU, bias=bias[:, i : i + 1], scale=1.0)
            relus[i] = relu

        def turn_back(i):
            planes = relus[i].shape[1]
            back = flip_pool.tile([P, planes, P], F32, name="back%d" % i, tag="bank")
            for m in range(planes):
                nc.tensor.transpose(back[:, m, :], relus[i][:, m, :], identity[:])
            backs[i] = back

        def divide(i, engine):
            planes = relus[i].shape[1]
            result = work.tile([P, planes, P], F32, name="result%d" % i, bufs=2 if i == 0 else 1)
            if engine == "vector":
                nc.vector.tensor_scalar_mul(result[:], backs[i][:], 1.0 / SCALES[i])
            else:
                nc.scalar.mul(out=result[:], in_=backs[i][:], mul=1.0 / SCALES[i])
            results[i] = result

        def store(b, i, first_plane=0):
            r = SCALES[i]
            first_row = (b * QUAD if r <= QUAD else 0) + first_plane
            if r == 1:
                rows = slice(first_row, first_row + results[i].shape[1])
                nc.sync.dma_start(out=out_rows[:, i, rows, :], in_=results[i][:])
                return
            for m in range(results[i].shape[1]):
                rows = slice(first_row + m * r, first_row + (m + 1) * r)
                nc.sync.dma_start(
                    out=out_rows[:, i, rows, :], in_=results[i][:, m : m + 1, :].to_broadcast([P, r, P])
                )

        last = len(units) - 1

        def is_x(n, tensor_sums=None):
            if not 0 <= n <= last or units[n][0] != "x":
                return False
            return tensor_sums is None or sums_on_tensor(*units[n][1:]) == tensor_sums

        fours = {}
        for n in range(len(units)):
            if is_x(n) and units[n][2] == N_UNITS - 1:
                fours[n if sums_on_tensor(*units[n][1:]) else n + 4] = units[n][1]

        with tc.manual_schedule():
            load(0)
            start_constants()
            for n in range(1, AHEAD):
                load(n)
            for n in range(-LEAD, last + 1):
                if n + LEAD > 0 and n + LEAD + AHEAD - 1 <= last:
                    load(n + LEAD + AHEAD - 1)
                done = n - 3
                finished = is_x(done) and units[done][2] == N_UNITS - 1
                if finished:
                    for i in range(2):
                        apply_relu(i, "scalar")
                if n - 1 in fours:
                    apply_relu(2, "scalar")
                if n + LEAD <= last:
                    transpose(n + LEAD)
                    copy_out(n + LEAD)
                if is_x(n - 1, False):
                    round_fours(n - 1)
                if n == 1 - LEAD:
                    finish_constants()
                if is_x(n + LEAD, True):
                    add_quads(n + LEAD)
                    round_quads(n + LEAD)
                if is_x(n + LEAD, False):
                    add_from_psum(n + LEAD)
                if n == last - 1:
                    quantise_quads(last)
                if is_x(n):
                    add_pairs(n)
                    if is_x(n, False):
                        add_fours(n)
                    quantise_rows(n)
                elif n >= 0:
                    quantise_weights(n)
                if is_x(n - 3, False):
                    quantise_quads(n - 3)
                if is_x(n - 1, False):
                    quantise_pairs(n - 1)
                if is_x(n + 1, True) and n + 1 < last:
                    quantise_quads(n + 1)
                if is_x(n, True):
                    quantise_pairs(n)
                if is_x(n + LEAD, True):
                    carry_quads(n + LEAD)
                if n == last:
                    multiply12()
                    apply_relu(3, "scalar")
                if n in fours:
                    multiply4(fours[n])
                if is_x(n - 2):
                    for i in range(2):
                        multiply(n - 2, i)
                if finished:
                    for i in range(2):
                        turn_back(i)
                    for i in range(2):
                        divide(i, "scalar")
                    for i in range(2):
                        store(units[done][1], i)
                if n - 1 in fours:
                    turn_back(2)
                    divide(2, "scalar")
                    store(fours[n - 1], 2)
            apply_relu(2, "scalar")
            for i in (3, 2):
                turn_back(i)
                divide(i, "scalar")
                store(N_BLOCKS - 1, i)
            for n in (last - 1, last):
                for i in range(2):
                    multiply(n, i)
            halves = (slice(0, QUAD // 2), slice(QUAD // 2, QUAD))
            parts = []
            for part in halves:
                apply_relu(0, "scalar", part)
                parts.append(relus[0])
            apply_relu(1, "vector")
            for part, relu in zip(halves, parts):
                relus[0] = relu
                turn_back(0)
                divide(0, "scalar")
                store(N_BLOCKS - 1, 0, part.start)
            turn_back(1)
            divide(1, "vector")
            store(N_BLOCKS - 1, 1)
